import numpy as np
import ml_dtypes


def mxq(x, axis, fmt="e4m3"):
    dtype, down = {"e4m3": (ml_dtypes.float8_e4m3fn, 7), "e5m2": (ml_dtypes.float8_e5m2, 14)}[fmt]
    v = np.moveaxis(np.asarray(x, np.float32).astype(ml_dtypes.bfloat16).astype(np.float64), axis, -1)
    blocks = v.reshape(v.shape[:-1] + (-1, 32))
    amax = np.abs(blocks).max(-1, keepdims=True)
    byte = np.maximum(np.where(amax > 0, np.frexp(amax)[1] - 1 + 127, 0) - down, 1)
    scale = np.exp2(byte - 127.0)
    codes = (blocks / scale).astype(np.float32).astype(dtype).astype(np.float64)
    return np.moveaxis((codes * scale).reshape(v.shape), -1, axis)


WIDE = False


def mx_kscale(k):
    if not WIDE:
        return np.ones(k)
    levels = np.array([10, -10, 5, -5, 0])
    if k % 512:
        return np.exp2(np.random.permutation(np.resize(levels, k // 32))).repeat(32)
    a = np.empty((k // 512, 16))
    for p in range(k // 512):
        a[p, :8] = np.random.permutation(np.resize(levels, 8))
        for g in range(8):
            far = levels[np.abs(levels - a[p, g]) >= 10]
            a[p, g + 8] = far[np.random.randint(len(far))]
    return np.exp2(a.ravel()).repeat(32)


BF16 = ml_dtypes.bfloat16


def bf(x):
    return np.asarray(x, np.float32).astype(BF16)


def f64(x):
    return np.asarray(x).astype(np.float64)


DIN, NH, HD, F, H, W, NFPB, LOCAL, SINK = 1024, 8, 128, 8, 16, 16, 2, 4, 2
DIM = NH * HD
C = HD // 2
S = F * H * W
TL = max(F, H, W)
EPS = 1e-06


def rms_norm(y, g):
    return y * (1.0 / np.sqrt(np.mean(y * y, axis=-1, keepdims=True) + EPS)) * g


def pos_table(tab):
    cf = C - 2 * (C // 3)
    ch = C // 3
    tf = np.broadcast_to(tab[:F, :cf][:, None, None, :], (F, H, W, cf))
    th = np.broadcast_to(tab[:H, cf:cf + ch][None, :, None, :], (F, H, W, ch))
    tw = np.broadcast_to(tab[:W, cf + ch:][None, None, :, :], (F, H, W, ch))
    return np.concatenate([tf, th, tw], axis=-1).reshape(S, C)


def rope(y, cosp, sinp):
    yp = y.reshape(S, NH, C, 2)
    yr, yi = yp[..., 0], yp[..., 1]
    cp, sp = cosp[:, None, :], sinp[:, None, :]
    return np.stack([yr * cp - yi * sp, yr * sp + yi * cp], axis=-1).reshape(S, NH, HD)


def draw0():
    s = mx_kscale(DIN)
    sc = 1.0 / np.sqrt(DIN)
    ang = np.random.uniform(0.0, 2.0 * np.pi, (TL, C))
    return {"x": bf(np.random.standard_normal((S, DIN)) * s),
            "Wq": bf(np.random.standard_normal((DIM, DIN)) * sc / s),
            "bq": bf(np.random.standard_normal(DIM) * 0.2),
            "Wk": bf(np.random.standard_normal((DIM, DIN)) * sc / s),
            "bk": bf(np.random.standard_normal(DIM) * 0.2),
            "gq": bf(1.4 * (1.0 + 0.1 * np.random.standard_normal(DIM))),
            "gk": bf(1.4 * (1.0 + 0.1 * np.random.standard_normal(DIM))),
            "freqs_cos": bf(np.cos(ang)), "freqs_sin": bf(np.sin(ang))}


def core(x, Wq, bq, Wk, bk, gq, gk, freqs_cos, freqs_sin):
    xq = mxq(f64(x), 1, "e4m3")
    q = rms_norm((xq @ mxq(f64(Wq), 1, "e4m3").T) + f64(bq), f64(gq))
    k = rms_norm((xq @ mxq(f64(Wk), 1, "e4m3").T) + f64(bk), f64(gk))
    cosp = pos_table(f64(freqs_cos))
    sinp = pos_table(f64(freqs_sin))
    return rope(q, cosp, sinp), rope(k, cosp, sinp)


def e4m3fn_bytes(y):
    return np.clip(np.asarray(y, np.float64), -448.0, 448.0).astype(np.float32).astype(ml_dtypes.float8_e4m3fn).view(np.uint8)


def e4m3fn_values(b):
    return np.asarray(b, np.uint8).view(ml_dtypes.float8_e4m3fn).astype(np.float64)


def setup_inputs():
    d = draw0()
    x0 = np.asarray(d['x']).astype(np.float64)
    s = (np.max(np.abs(x0), axis=(0,), keepdims=True) / 448.0).astype(np.float32)
    out = {}
    for k, v in d.items():
        if k == 'x':
            out['x_bytes'] = e4m3fn_bytes(x0 / s.astype(np.float64))
            out['x_scale'] = s
        else:
            out[k] = v
    return out


def reference(x_bytes, x_scale, Wq, bq, Wk, bk, gq, gk, freqs_cos, freqs_sin):
    return core(e4m3fn_values(x_bytes) * x_scale.astype(np.float64), Wq, bq, Wk, bk, gq, gk, freqs_cos, freqs_sin)

@@ -1,0 +1,255 @@
+from contextlib import ExitStack
+
+import concourse.mybir as mybir
+from concourse.masks import make_identity
+
+F32 = mybir.dt.float32
+BF16 = mybir.dt.bfloat16
+U32 = mybir.dt.uint32
+U8 = mybir.dt.uint8
+FP8 = mybir.dt.float8_e4m3fn
+FP8X4 = mybir.dt.float8_e4m3fn_x4
+ALU = mybir.AluOpType
+ACT = mybir.ActivationFunctionType
+
+P = 128
+KDIM = 1024
+CHUNK = 512
+NCHUNK = 4
+EPS = 1e-06
+
+FLOPS = 2 * 2048 * 2048 * 1024
+
+
+def tile_causalwanselfattention_pa_kernel(
+    tc, x_bytes, x_scale, Wq, bq, Wk, bk, gq, gk, freqs_cos, freqs_sin, out_0, out_1
+):
+    nc = tc.nc
+    outs = (out_0.rearrange("t n d -> t (n d)"), out_1.rearrange("t n d -> t (n d)"))
+    weights = (Wq, Wk)
+
+    with ExitStack() as ctx:
+        const = ctx.enter_context(tc.tile_pool(name="const", bufs=1))
+        keep = ctx.enter_context(tc.tile_pool(name="keep", bufs=1))
+        stage = ctx.enter_context(tc.tile_pool(name="stage", bufs=2))
+        ypool = ctx.enter_context(tc.tile_pool(name="ypool", bufs=2))
+        work = ctx.enter_context(tc.tile_pool(name="work", bufs=3))
+        stats = ctx.enter_context(tc.tile_pool(name="stats", bufs=2))
+        ps = ctx.enter_context(tc.psum_pool(name="ps", bufs=2))
+
+        brow = const.tile([P, P], BF16)
+        nc.vector.memset(brow[:], 0.0)
+        raw = const.tile([P, P], BF16)
+        nc.vector.memset(raw[:], 0.0)
+        sgn = const.tile([P, 2], F32)
+        nc.vector.memset(sgn[:, 0:1], 1.0)
+        nc.vector.memset(sgn[:, 1:2], -1.0)
+        identf = const.tile([P, P], F32)
+        make_identity(nc, identf[:])
+        identb = const.tile([P, P], BF16)
+        make_identity(nc, identb[:])
+
+        for r, vec in enumerate((bq, bk, gq, gk)):
+            nc.scalar.dma_start(out=brow[8 * r:8 * r + 8, :], in_=vec.rearrange("(m p) -> m p", p=P))
+        for half, tabl in enumerate((freqs_cos, freqs_sin)):
+            for r0, c0, c1 in ((0, 0, 22), (32, 22, 43), (64, 43, 64)):
+                nc.scalar.dma_start(out=raw[r0:r0 + 16, 64 * half + c0:64 * half + c1], in_=tabl[:, c0:c1])
+
+        xb = []
+        wraw = []
+
+        def load_x(c):
+            xb_c = keep.tile([P, 4, KDIM], U8, name="xb%d" % c)
+            nc.sync.dma_start(
+                out=xb_c[:], in_=x_bytes[CHUNK * c:CHUNK * (c + 1), :].rearrange("(i p) k -> p i k", p=P)
+            )
+            xb.append(xb_c)
+
+        def load_w(j):
+            w = weights[j // 4]
+            r0 = 256 * (j % 4)
+            wr = stage.tile([P, 2, KDIM], BF16, tag="wraw", bufs=6, name="wraw")
+            nc.sync.dma_start(out=wr[:], in_=w[r0:r0 + 256, :].rearrange("(m p) k -> p m k", p=P))
+            wraw.append(wr)
+
+        load_x(0)
+        sc_bc = const.tile([P, KDIM], F32)
+        nc.sync.dma_start(out=sc_bc[:], in_=x_scale.rearrange("o k -> (o k)").partition_broadcast(P))
+        load_w(0)
+        load_w(1)
+        load_x(1)
+        load_w(2)
+        load_w(3)
+        load_x(2)
+        load_w(4)
+        load_w(5)
+        load_x(3)
+
+        xc = keep.tile([P, NCHUNK, 2, CHUNK], U32, align_bytes=64)
+        xs = keep.tile([P, NCHUNK, 2, CHUNK], U8, align_bytes=64)
+        wc = keep.tile([P, 4, 2, CHUNK], U32, align_bytes=64)
+        ws = keep.tile([P, 4, 2, CHUNK], U8, align_bytes=64)
+
+        def turn(rows_bf16, grp, slot):
+            words = rows_bf16.bitcast(F32)
+            ft = ps.tile([P, 4, P], F32, tag="ft", bufs=2, name="ft")
+            for g in range(2):
+                for u in range(2):
+                    nc.tensor.transpose(ft[:, 2 * g + u, :], words[:, 256 * g + u:256 * (g + 1):2], identf[:])
+            nc.scalar.copy(
+                out=grp[:].bitcast(F32)[:, :, P * slot:P * (slot + 1), :],
+                in_=ft[:].rearrange("p (g u) r -> p g r u", u=2),
+            )
+
+        def quantize(grp, codes, scales):
+            nc.vector.quantize_mx(
+                out=codes.rearrange("p g n -> p (g n)").bitcast(FP8X4),
+                scales=scales.rearrange("p g n -> p (g n)"),
+                in_=grp[:].rearrange("p g r t -> p (g r t)"),
+            )
+
+        def front_x(c):
+            xg = stage.tile([P, 2, CHUNK, 4], BF16, tag="grp", bufs=2, align_bytes=64, name="xgrp")
+            for i in range(4):
+                xw = stage.tile([P, KDIM], BF16, tag="xw", bufs=3, name="xw")
+                nc.vector.tensor_tensor(out=xw[:], in0=xb[c][:, i, :].bitcast(FP8), in1=sc_bc[:], op=ALU.mult)
+                turn(xw[:], xg, i)
+            quantize(xg, xc[:, c], xs[:, c])
+
+        def front_w(q4):
+            wg = stage.tile([P, 2, CHUNK, 4], BF16, tag="grp", bufs=2, align_bytes=64, name="wgrp")
+            for mm in range(4):
+                turn(wraw[2 * q4 + mm // 2][:, mm % 2, :], wg, mm)
+            quantize(wg, wc[:, q4], ws[:, q4])
+
+        front_x(0)
+        front_w(0)
+        front_w(1)
+        load_w(6)
+        load_w(7)
+
+        psb = ps.tile([P, P], BF16, tag="ft", bufs=2, name="psb")
+        nc.tensor.transpose(psb[:], brow[:], identb[:])
+        cols = const.tile([P, 32], F32)
+        nc.vector.tensor_copy(out=cols[:], in_=psb[:, 0:32])
+        gbcol = const.tile([P, 16], F32)
+        nc.vector.tensor_tensor(out=gbcol[:], in0=cols[:, 0:16], in1=cols[:, 16:32], op=ALU.mult)
+
+        zT = {}
+        sq = {}
+        rstd = {}
+
+        def stage_a(unit, mm):
+            c, qk = unit // 2, unit % 2
+            m = 8 * qk + mm
+            q4, m4 = m // 4, m % 4
+            acc = ps.tile([P, CHUNK], F32, tag="acc", bufs=2, name="acc")
+            for g in range(2):
+                nc.tensor.matmul_mx(
+                    out=acc[:],
+                    lhsT=wc[:, q4, g, P * m4:P * (m4 + 1)].bitcast(FP8X4),
+                    lhsT_scale=ws[:, q4, g, P * m4:P * (m4 + 1)],
+                    rhs=xc[:, c, g, :].bitcast(FP8X4),
+                    rhs_scale=xs[:, c, g, :],
+                    start=(g == 0),
+                    stop=(g == 1),
+                )
+            s2 = ypool.tile([P, CHUNK], F32, tag="sq%d" % mm, bufs=2, name="sq%d" % mm)
+            nc.scalar.activation(out=s2[:], in_=acc[:], func=ACT.Square, bias=cols[:, m:m + 1], scale=1.0)
+            zt = ypool.tile([P, CHUNK], F32, tag="zT%d" % mm, bufs=2, name="zT%d" % mm)
+            nc.scalar.activation(
+                out=zt[:], in_=acc[:], func=ACT.Identity, bias=gbcol[:, m:m + 1], scale=cols[:, 16 + m:17 + m]
+            )
+            sq[(unit, mm)] = s2
+            zT[(unit, mm)] = zt
+
+        def norms(unit):
+            accq = ps.tile([P, 4, P], F32, tag="ft", bufs=2, name="accq")
+            for ii in range(4):
+                for mm in range(8):
+                    nc.tensor.matmul(
+                        out=accq[:, ii, :], lhsT=sq[(unit, mm)][:, P * ii:P * (ii + 1)], rhs=identf[:],
+                        is_transpose=True, start=(mm == 0), stop=(mm == 7),
+                    )
+            ssq = stats.tile([P, 4], F32, name="ssq")
+            nc.vector.tensor_reduce(out=ssq[:], in_=accq[:], axis=mybir.AxisListType.X, op=ALU.add)
+            ms = stats.tile([P, 4], F32, name="ms")
+            nc.vector.tensor_scalar(
+                out=ms[:], in0=ssq[:], scalar1=1024.0 * EPS, scalar2=1.0 / 1024.0, op0=ALU.add, op1=ALU.mult
+            )
+            sd = stats.tile([P, 4], F32, name="sd")
+            nc.scalar.activation(out=sd[:], in_=ms[:], func=ACT.Sqrt)
+            rs = stats.tile([P, 4], F32, name="rs")
+            nc.vector.reciprocal(out=rs[:], in_=sd[:])
+            rstd[unit] = rs
+
+        for mm in range(8):
+            stage_a(0, mm)
+        norms(0)
+
+        ftx = const.tile([P, 2, 64, 2], BF16)
+        nc.vector.tensor_copy(out=ftx[:, 0], in_=raw[:, 0:64].unsqueeze(2).to_broadcast([P, 64, 2]))
+        nc.vector.tensor_tensor(
+            out=ftx[:, 1], in0=raw[:, 64:128].unsqueeze(2).to_broadcast([P, 64, 2]),
+            in1=sgn[:].unsqueeze(1).to_broadcast([P, 64, 2]), op=ALU.mult,
+        )
+        base = []
+        for hh in range(2):
+            bs = const.tile([P, 8, 16], BF16, name="base%d" % hh)
+            nc.vector.tensor_tensor(
+                out=bs[:], in0=identb[:, 32 + 8 * hh:40 + 8 * hh].unsqueeze(2).to_broadcast([P, 8, 16]),
+                in1=identb[:, 64:80].unsqueeze(1).to_broadcast([P, 8, 16]), op=ALU.add,
+            )
+            base.append(bs)
+        tab = const.tile([P, 16, 256], F32)
+        ftx2 = ftx[:].rearrange("k a c e -> k (a c e)")
+        for f in range(8):
+            pt = ps.tile([P, 2, 256], F32, tag="yN", bufs=4, name="pt")
+            for hh in range(2):
+                nc.tensor.matmul(
+                    out=pt[:, hh, :], lhsT=identb[:, f:f + 1].to_broadcast([P, P]), rhs=ftx2, start=True, stop=False
+                )
+                nc.tensor.matmul(
+                    out=pt[:, hh, :], lhsT=base[hh][:].rearrange("k a b -> k (a b)"), rhs=ftx2, start=False, stop=True
+                )
+            nc.scalar.copy(out=tab[:, 2 * f:2 * f + 2, :], in_=pt[:])
+
+        front_x(1)
+        front_w(2)
+        front_w(3)
+        front_x(2)
+        front_x(3)
+
+        def stage_b(unit, ii):
+            c, qk = unit // 2, unit % 2
+            i = 4 * c + ii
+            u = work.tile([P, 8, P], F32, tag="u", bufs=3, name="u")
+            v = work.tile([P, 8, P], F32, tag="v", bufs=3, name="v")
+            o = work.tile([P, 8, P], F32, tag="o", bufs=3, name="o")
+            for b in range(2):
+                yn = ps.tile([P, 4, P], F32, tag="yN", bufs=4, name="yN")
+                for j in range(4):
+                    nc.tensor.transpose(yn[:, j, :], zT[(unit, 4 * b + j)][:, P * ii:P * (ii + 1)], identf[:])
+                hs = slice(4 * b, 4 * b + 4)
+                for dst, t0 in ((u, 0), (v, P)):
+                    nc.vector.scalar_tensor_tensor(
+                        out=dst[:, hs, :], in0=yn[:], scalar=rstd[unit][:, ii:ii + 1],
+                        in1=tab[:, i, t0:t0 + P].unsqueeze(1).to_broadcast([P, 4, P]),
+                        op0=ALU.mult, op1=ALU.mult,
+                    )
+                nc.gpsimd.tensor_tensor(
+                    out=o[:, hs, :].rearrange("p h (c e) -> p (h c) e", e=2),
+                    in0=u[:, hs, :].rearrange("p h (c e) -> p (h c) e", e=2),
+                    in1=v[:, hs, :].rearrange("p h (c e) -> p (h c) e", e=2)[:, :, ::-1],
+                    op=ALU.add,
+                )
+            nc.sync.dma_start(out=outs[qk][P * i:P * (i + 1), :], in_=o[:].rearrange("p h j -> p (h j)"))
+
+        for unit in range(8):
+            for ii in range(4):
+                stage_b(unit, ii)
+                if unit + 1 < 8:
+                    stage_a(unit + 1, 2 * ii)
+                    stage_a(unit + 1, 2 * ii + 1)
+            if unit + 1 < 8:
+                norms(unit + 1)

@@ -16,7 +16,13 @@ P = 128
 KDIM = 1024
 CHUNK = 512
 NCHUNK = 4
+NH = 8
 EPS = 1e-06
+FR = 44
+HR = 84
+FW = NH * FR
+HWW = NH * HR
+SCR = 1920
 
 FLOPS = 2 * 2048 * 2048 * 1024
 
@@ -33,14 +39,14 @@ def tile_causalwanselfattention_pa_kernel(
         keep = ctx.enter_context(tc.tile_pool(name="keep", bufs=1))
         stage = ctx.enter_context(tc.tile_pool(name="stage", bufs=2))
         ypool = ctx.enter_context(tc.tile_pool(name="ypool", bufs=2))
-        work = ctx.enter_context(tc.tile_pool(name="work", bufs=3))
-        stats = ctx.enter_context(tc.tile_pool(name="stats", bufs=2))
+        work = ctx.enter_context(tc.tile_pool(name="work", bufs=2))
+        stats = ctx.enter_context(tc.tile_pool(name="stats", bufs=4))
         ps = ctx.enter_context(tc.psum_pool(name="ps", bufs=2))
 
-        brow = const.tile([P, P], BF16)
-        nc.vector.memset(brow[:], 0.0)
         raw = const.tile([P, P], BF16)
         nc.vector.memset(raw[:], 0.0)
+        bz = const.tile([P, 2 * KDIM], BF16)
+        nc.vector.memset(bz[:], 0.0)
         sgn = const.tile([P, 2], F32)
         nc.vector.memset(sgn[:, 0:1], 1.0)
         nc.vector.memset(sgn[:, 1:2], -1.0)
@@ -49,143 +55,84 @@ def tile_causalwanselfattention_pa_kernel(
         identb = const.tile([P, P], BF16)
         make_identity(nc, identb[:])
 
-        for r, vec in enumerate((bq, bk, gq, gk)):
-            nc.scalar.dma_start(out=brow[8 * r:8 * r + 8, :], in_=vec.rearrange("(m p) -> m p", p=P))
         for half, tabl in enumerate((freqs_cos, freqs_sin)):
             for r0, c0, c1 in ((0, 0, 22), (32, 22, 43), (64, 43, 64)):
                 nc.scalar.dma_start(out=raw[r0:r0 + 16, 64 * half + c0:64 * half + c1], in_=tabl[:, c0:c1])
+        for qk, vec in enumerate((bq, bk)):
+            v3 = vec.rearrange("(o h r) -> o h r", o=1, r=P)
+            nc.scalar.dma_start(
+                out=bz[0:1, KDIM * qk:KDIM * qk + FW].rearrange("o (h r) -> o h r", r=FR), in_=v3[:, :, 0:FR]
+            )
+            nc.scalar.dma_start(
+                out=bz[0:1, KDIM * qk + FW:KDIM * (qk + 1)].rearrange("o (h r) -> o h r", r=HR), in_=v3[:, :, FR:P]
+            )
 
-        xb = []
-        wraw = []
+        xb = {}
+        wraw = {}
 
         def load_x(c):
-            xb_c = keep.tile([P, 4, KDIM], U8, name="xb%d" % c)
+            xb_c = stage.tile([P, 4, KDIM], U8, tag="xb", bufs=2, name="xb")
             nc.sync.dma_start(
                 out=xb_c[:], in_=x_bytes[CHUNK * c:CHUNK * (c + 1), :].rearrange("(i p) k -> p i k", p=P)
             )
-            xb.append(xb_c)
+            xb[c] = xb_c
 
         def load_w(j):
             w = weights[j // 4]
             r0 = 256 * (j % 4)
-            wr = stage.tile([P, 2, KDIM], BF16, tag="wraw", bufs=6, name="wraw")
+            wr = stage.tile([P, 2, KDIM], BF16, tag="wraw", bufs=4, name="wraw")
             nc.sync.dma_start(out=wr[:], in_=w[r0:r0 + 256, :].rearrange("(m p) k -> p m k", p=P))
-            wraw.append(wr)
+            wraw[j] = wr
 
+        gbc = const.tile([P, 2, KDIM], BF16)
         load_x(0)
         sc_bc = const.tile([P, KDIM], F32)
         nc.sync.dma_start(out=sc_bc[:], in_=x_scale.rearrange("o k -> (o k)").partition_broadcast(P))
-        load_w(0)
-        load_w(1)
+        nc.sync.dma_start(out=gbc[:, 0, :], in_=gq.partition_broadcast(P))
+        for j in range(4):
+            load_w(j)
+        nc.sync.dma_start(out=gbc[:, 1, :], in_=gk.partition_broadcast(P))
         load_x(1)
-        load_w(2)
-        load_w(3)
-        load_x(2)
-        load_w(4)
-        load_w(5)
-        load_x(3)
 
         xc = keep.tile([P, NCHUNK, 2, CHUNK], U32, align_bytes=64)
         xs = keep.tile([P, NCHUNK, 2, CHUNK], U8, align_bytes=64)
-        wc = keep.tile([P, 4, 2, CHUNK], U32, align_bytes=64)
-        ws = keep.tile([P, 4, 2, CHUNK], U8, align_bytes=64)
+        wc = keep.tile([P, 2, 2, KDIM], U32, align_bytes=64)
+        ws = keep.tile([P, 2, 2, KDIM], U8, align_bytes=64)
 
-        def turn(rows_bf16, grp, slot):
+        def turn(rows_bf16):
             words = rows_bf16.bitcast(F32)
-            ft = ps.tile([P, 4, P], F32, tag="ft", bufs=2, name="ft")
+            ft = ps.tile([P, 4, P], F32, tag="acc", bufs=2, name="ft")
             for g in range(2):
                 for u in range(2):
                     nc.tensor.transpose(ft[:, 2 * g + u, :], words[:, 256 * g + u:256 * (g + 1):2], identf[:])
-            nc.scalar.copy(
-                out=grp[:].bitcast(F32)[:, :, P * slot:P * (slot + 1), :],
-                in_=ft[:].rearrange("p (g u) r -> p g r u", u=2),
-            )
-
-        def quantize(grp, codes, scales):
-            nc.vector.quantize_mx(
-                out=codes.rearrange("p g n -> p (g n)").bitcast(FP8X4),
-                scales=scales.rearrange("p g n -> p (g n)"),
-                in_=grp[:].rearrange("p g r t -> p (g r t)"),
-            )
+            return ft[:].rearrange("p (g u) r -> p g r u", u=2)
 
         def front_x(c):
-            xg = stage.tile([P, 2, CHUNK, 4], BF16, tag="grp", bufs=2, align_bytes=64, name="xgrp")
+            xg = stage.tile([P, 2, CHUNK, 4], BF16, tag="xg", bufs=2, align_bytes=64, name="xg")
             for i in range(4):
                 xw = stage.tile([P, KDIM], BF16, tag="xw", bufs=3, name="xw")
                 nc.vector.tensor_tensor(out=xw[:], in0=xb[c][:, i, :].bitcast(FP8), in1=sc_bc[:], op=ALU.mult)
-                turn(xw[:], xg, i)
-            quantize(xg, xc[:, c], xs[:, c])
+                ftv = turn(xw[:])
+                nc.scalar.copy(out=xg[:].bitcast(F32)[:, :, P * i:P * (i + 1), :], in_=ftv)
+            nc.vector.quantize_mx(
+                out=xc[:, c].rearrange("p g n -> p (g n)").bitcast(FP8X4),
+                scales=xs[:, c].rearrange("p g n -> p (g n)"),
+                in_=xg[:].rearrange("p g r t -> p (g r t)"),
+            )
 
-        def front_w(q4):
-            wg = stage.tile([P, 2, CHUNK, 4], BF16, tag="grp", bufs=2, align_bytes=64, name="wgrp")
-            for mm in range(4):
-                turn(wraw[2 * q4 + mm // 2][:, mm % 2, :], wg, mm)
-            quantize(wg, wc[:, q4], ws[:, q4])
-
-        front_x(0)
-        front_w(0)
-        front_w(1)
-        load_w(6)
-        load_w(7)
-
-        psb = ps.tile([P, P], BF16, tag="ft", bufs=2, name="psb")
-        nc.tensor.transpose(psb[:], brow[:], identb[:])
-        cols = const.tile([P, 32], F32)
-        nc.vector.tensor_copy(out=cols[:], in_=psb[:, 0:32])
-        gbcol = const.tile([P, 16], F32)
-        nc.vector.tensor_tensor(out=gbcol[:], in0=cols[:, 0:16], in1=cols[:, 16:32], op=ALU.mult)
-
-        zT = {}
-        sq = {}
-        rstd = {}
-
-        def stage_a(unit, mm):
-            c, qk = unit // 2, unit % 2
-            m = 8 * qk + mm
-            q4, m4 = m // 4, m % 4
-            acc = ps.tile([P, CHUNK], F32, tag="acc", bufs=2, name="acc")
+        def front_w(qk):
+            wg = stage.tile([P, 2, KDIM, 4], BF16, tag="wg", bufs=1, align_bytes=64, name="wg")
+            wgw = wg[:].bitcast(F32)
+            for h in range(NH):
+                ftv = turn(wraw[4 * qk + h // 2][:, h % 2, :])
+                nc.scalar.copy(out=wgw[:, :, FR * h:FR * (h + 1), :], in_=ftv[:, :, 0:FR, :])
+                nc.scalar.copy(out=wgw[:, :, FW + HR * h:FW + HR * (h + 1), :], in_=ftv[:, :, FR:P, :])
             for g in range(2):
-                nc.tensor.matmul_mx(
-                    out=acc[:],
-                    lhsT=wc[:, q4, g, P * m4:P * (m4 + 1)].bitcast(FP8X4),
-                    lhsT_scale=ws[:, q4, g, P * m4:P * (m4 + 1)],
-                    rhs=xc[:, c, g, :].bitcast(FP8X4),
-                    rhs_scale=xs[:, c, g, :],
-                    start=(g == 0),
-                    stop=(g == 1),
+                nc.vector.quantize_mx(
+                    out=wc[:, qk, g, :].bitcast(FP8X4),
+                    scales=ws[:, qk, g, :],
+                    in_=wg[:, g].rearrange("p r t -> p (r t)"),
                 )
-            s2 = ypool.tile([P, CHUNK], F32, tag="sq%d" % mm, bufs=2, name="sq%d" % mm)
-            nc.scalar.activation(out=s2[:], in_=acc[:], func=ACT.Square, bias=cols[:, m:m + 1], scale=1.0)
-            zt = ypool.tile([P, CHUNK], F32, tag="zT%d" % mm, bufs=2, name="zT%d" % mm)
-            nc.scalar.activation(
-                out=zt[:], in_=acc[:], func=ACT.Identity, bias=gbcol[:, m:m + 1], scale=cols[:, 16 + m:17 + m]
-            )
-            sq[(unit, mm)] = s2
-            zT[(unit, mm)] = zt
-
-        def norms(unit):
-            accq = ps.tile([P, 4, P], F32, tag="ft", bufs=2, name="accq")
-            for ii in range(4):
-                for mm in range(8):
-                    nc.tensor.matmul(
-                        out=accq[:, ii, :], lhsT=sq[(unit, mm)][:, P * ii:P * (ii + 1)], rhs=identf[:],
-                        is_transpose=True, start=(mm == 0), stop=(mm == 7),
-                    )
-            ssq = stats.tile([P, 4], F32, name="ssq")
-            nc.vector.tensor_reduce(out=ssq[:], in_=accq[:], axis=mybir.AxisListType.X, op=ALU.add)
-            ms = stats.tile([P, 4], F32, name="ms")
-            nc.vector.tensor_scalar(
-                out=ms[:], in0=ssq[:], scalar1=1024.0 * EPS, scalar2=1.0 / 1024.0, op0=ALU.add, op1=ALU.mult
-            )
-            sd = stats.tile([P, 4], F32, name="sd")
-            nc.scalar.activation(out=sd[:], in_=ms[:], func=ACT.Sqrt)
-            rs = stats.tile([P, 4], F32, name="rs")
-            nc.vector.reciprocal(out=rs[:], in_=sd[:])
-            rstd[unit] = rs
-
-        for mm in range(8):
-            stage_a(0, mm)
-        norms(0)
 
         ftx = const.tile([P, 2, 64, 2], BF16)
         nc.vector.tensor_copy(out=ftx[:, 0], in_=raw[:, 0:64].unsqueeze(2).to_broadcast([P, 64, 2]))
@@ -201,55 +148,174 @@ def tile_causalwanselfattention_pa_kernel(
                 in1=identb[:, 64:80].unsqueeze(1).to_broadcast([P, 8, 16]), op=ALU.add,
             )
             base.append(bs)
-        tab = const.tile([P, 16, 256], F32)
-        ftx2 = ftx[:].rearrange("k a c e -> k (a c e)")
-        for f in range(8):
-            pt = ps.tile([P, 2, 256], F32, tag="yN", bufs=4, name="pt")
-            for hh in range(2):
-                nc.tensor.matmul(
-                    out=pt[:, hh, :], lhsT=identb[:, f:f + 1].to_broadcast([P, P]), rhs=ftx2, start=True, stop=False
-                )
-                nc.tensor.matmul(
-                    out=pt[:, hh, :], lhsT=base[hh][:].rearrange("k a b -> k (a b)"), rhs=ftx2, start=False, stop=True
-                )
-            nc.scalar.copy(out=tab[:, 2 * f:2 * f + 2, :], in_=pt[:])
 
-        front_x(1)
-        front_w(2)
-        front_w(3)
-        front_x(2)
-        front_x(3)
+        front_x(0)
 
-        def stage_b(unit, ii):
-            c, qk = unit // 2, unit % 2
-            i = 4 * c + ii
-            u = work.tile([P, 8, P], F32, tag="u", bufs=3, name="u")
-            v = work.tile([P, 8, P], F32, tag="v", bufs=3, name="v")
-            o = work.tile([P, 8, P], F32, tag="o", bufs=3, name="o")
-            for b in range(2):
-                yn = ps.tile([P, 4, P], F32, tag="yN", bufs=4, name="yN")
-                for j in range(4):
-                    nc.tensor.transpose(yn[:, j, :], zT[(unit, 4 * b + j)][:, P * ii:P * (ii + 1)], identf[:])
-                hs = slice(4 * b, 4 * b + 4)
-                for dst, t0 in ((u, 0), (v, P)):
-                    nc.vector.scalar_tensor_tensor(
-                        out=dst[:, hs, :], in0=yn[:], scalar=rstd[unit][:, ii:ii + 1],
-                        in1=tab[:, i, t0:t0 + P].unsqueeze(1).to_broadcast([P, 4, P]),
-                        op0=ALU.mult, op1=ALU.mult,
+        pt = ps.tile([P, 2, 256], F32, tag="acc", bufs=2, name="pt")
+        for hh in range(2):
+            nc.tensor.matmul(
+                out=pt[:, hh, :], lhsT=base[hh][:].rearrange("k a b -> k (a b)"),
+                rhs=ftx[:].rearrange("k a c e -> k (a c e)"), start=True, stop=True,
+            )
+        tabs = const.tile([P, 2, 2, P], BF16)
+        nc.scalar.copy(out=tabs[:].rearrange("p s a r -> p s (a r)"), in_=pt[:])
+
+        pb = ps.tile([P, 16], F32, tag="acc", bufs=2, name="pb")
+        for idx in range(16):
+            nc.tensor.matmul(
+                out=pb[:, idx:idx + 1], lhsT=bz[:, P * idx:P * (idx + 1)], rhs=identb[:, 0:1], start=True, stop=True
+            )
+        bcol = const.tile([P, 16], F32)
+        nc.vector.tensor_copy(out=bcol[:], in_=pb[:])
+
+        rf = const.tile([16, 2, 2 * FW], F32)
+        hwtab = const.tile([P, 2, 2, 2, HWW], F32)
+        gv = gbc[:].rearrange("p q (h r) -> p q h r", r=P)
+
+        def make_rf(qk):
+            nc.gpsimd.tensor_tensor(
+                out=rf[:, qk, :].rearrange("p (a h r) -> p a h r", a=2, r=FR),
+                in0=gv[0:16, qk, :, 0:FR].unsqueeze(1).to_broadcast([16, 2, NH, FR]),
+                in1=ftx[0:16].rearrange("p a c e -> p a (c e)")[:, :, 0:FR].unsqueeze(2).to_broadcast([16, 2, NH, FR]),
+                op=ALU.mult,
+            )
+            nc.sync.dma_start(out=outs[1][SCR + 16 * qk:SCR + 16 * qk + 16, 0:2 * FW], in_=rf[:, qk, :])
+
+        def make_hw(qk, hh):
+            nc.gpsimd.tensor_tensor(
+                out=hwtab[:, qk, hh].rearrange("p a (h r) -> p a h r", r=HR),
+                in0=gv[:, qk, :, FR:P].unsqueeze(1).to_broadcast([P, 2, NH, HR]),
+                in1=tabs[:, hh, :, FR:P].unsqueeze(2).to_broadcast([P, 2, NH, HR]),
+                op=ALU.mult,
+            )
+
+        ftab = {}
+
+        def load_ftab(c):
+            ft_c = work.tile([P, 2, 2, 2, FW], F32, tag="ftab", bufs=2, name="ftab")
+            for qk in range(2):
+                for f2 in range(2):
+                    nc.sync.dma_start(
+                        out=ft_c[:, f2, qk].rearrange("p a x -> p (a x)"),
+                        in_=outs[1][SCR + 16 * qk + 2 * c + f2:SCR + 16 * qk + 2 * c + f2 + 1, 0:2 * FW]
+                        .rearrange("o x -> (o x)").partition_broadcast(P),
                     )
+            ftab[c] = ft_c
+
+        make_rf(0)
+        make_hw(0, 0)
+        make_hw(0, 1)
+        make_rf(1)
+        make_hw(1, 0)
+        make_hw(1, 1)
+
+        front_w(0)
+        for j in range(4, 8):
+            load_w(j)
+        load_ftab(0)
+        load_x(2)
+
+        yT = {}
+
+        def stage_a(unit, m):
+            c, qk = unit // 2, unit % 2
+            acc = ps.tile([P, CHUNK], F32, tag="acc", bufs=2, name="acc")
+            for g in range(2):
+                nc.tensor.matmul_mx(
+                    out=acc[:],
+                    lhsT=wc[:, qk, g, P * m:P * (m + 1)].bitcast(FP8X4),
+                    lhsT_scale=ws[:, qk, g, P * m:P * (m + 1)],
+                    rhs=xc[:, c, g, :].bitcast(FP8X4),
+                    rhs_scale=xs[:, c, g, :],
+                    start=(g == 0),
+                    stop=(g == 1),
+                )
+            yt = ypool.tile([P, CHUNK], F32, tag="yT%d" % m, bufs=2, name="yT%d" % m)
+            nc.scalar.activation(
+                out=yt[:], in_=acc[:], func=ACT.Identity, bias=bcol[:, 8 * qk + m:8 * qk + m + 1], scale=1.0
+            )
+            yT[(unit, m)] = yt
+
+        yn = {}
+        rstd = {}
+
+        def t8(j):
+            unit, ii = j // 4, j % 4
+            banks = []
+            for b in range(2):
+                y = ps.tile([P, 4, P], F32, tag="yn", bufs=6, name="yn")
+                for mm in range(4):
+                    nc.tensor.transpose(y[:, mm, :], yT[(unit, 4 * b + mm)][:, P * ii:P * (ii + 1)], identf[:])
+                banks.append(y)
+            yn[j] = banks
+
+        def sq(j):
+            s2 = stats.tile([P, 2], F32, name="s2")
+            for b in range(2):
+                junk = work.tile([P, CHUNK], BF16, tag="junk", bufs=2, name="junk")
+                nc.scalar.activation(
+                    out=junk[:], in_=yn[j][b][:].rearrange("p m r -> p (m r)"), func=ACT.Square,
+                    scale=1.0 / 32.0, accum_out=s2[:, b:b + 1],
+                )
+            j2 = stats.tile([P, 2], F32, name="j2")
+            ms = stats.tile([P, 1], F32, name="ms")
+            nc.scalar.activation(out=j2[:], in_=s2[:], func=ACT.Identity, bias=0.5 * EPS, scale=1.0, accum_out=ms[:])
+            rs = stats.tile([P, 1], F32, name="rs")
+            nc.scalar.activation(out=rs[:], in_=ms[:], func=ACT.Abs_reciprocal_sqrt)
+            rstd[j] = rs
+
+        def rot(j):
+            unit, ii = j // 4, j % 4
+            c, qk = unit // 2, unit % 2
+            f2, hh = ii // 2, ii % 2
+            i = 4 * c + ii
+            y0 = yn[j][0][:].rearrange("p m r -> p (m r)")
+            y1 = yn[j][1][:].rearrange("p m r -> p (m r)")
+            uv = work.tile([P, 2, KDIM], F32, tag="uv", bufs=2, name="uv")
+            for src, lo, hi, tabv in (
+                (y0[:, 0:FW], 0, FW, ftab[c][:, f2, qk]),
+                (y0[:, FW:CHUNK], FW, CHUNK, hwtab[:, qk, hh, :, 0:CHUNK - FW]),
+                (y1, CHUNK, KDIM, hwtab[:, qk, hh, :, CHUNK - FW:HWW]),
+            ):
+                nc.vector.scalar_tensor_tensor(
+                    out=uv[:, :, lo:hi], in0=src.unsqueeze(1).to_broadcast([P, 2, hi - lo]),
+                    scalar=rstd[j][:, 0:1], in1=tabv, op0=ALU.mult, op1=ALU.mult,
+                )
+            o = work.tile([P, NH, P], F32, tag="o", bufs=3, name="o")
+            for lo, hi, r0, r1 in ((0, FW, 0, FR), (FW, KDIM, FR, P)):
                 nc.gpsimd.tensor_tensor(
-                    out=o[:, hs, :].rearrange("p h (c e) -> p (h c) e", e=2),
-                    in0=u[:, hs, :].rearrange("p h (c e) -> p (h c) e", e=2),
-                    in1=v[:, hs, :].rearrange("p h (c e) -> p (h c) e", e=2)[:, :, ::-1],
+                    out=o[:, :, r0:r1].rearrange("p h (c e) -> p h c e", e=2),
+                    in0=uv[:, 0, lo:hi].rearrange("p (h c e) -> p h c e", h=NH, e=2),
+                    in1=uv[:, 1, lo:hi].rearrange("p (h c e) -> p h c e", h=NH, e=2)[:, :, :, ::-1],
                     op=ALU.add,
                 )
-            nc.sync.dma_start(out=outs[qk][P * i:P * (i + 1), :], in_=o[:].rearrange("p h j -> p (h j)"))
+            nc.sync.dma_start(out=outs[qk][P * i:P * (i + 1), :], in_=o[:].rearrange("p h r -> p (h r)"))
 
-        for unit in range(8):
-            for ii in range(4):
-                stage_b(unit, ii)
-                if unit + 1 < 8:
-                    stage_a(unit + 1, 2 * ii)
-                    stage_a(unit + 1, 2 * ii + 1)
+        for m in range(8):
+            stage_a(0, m)
+        front_w(1)
+        front_x(1)
+        load_x(3)
+        load_ftab(1)
+        t8(0)
+        sq(0)
+
+        pieces = ((0, 1, 2), (3, 4, 5), (6, 7), ())
+        for j in range(32):
+            unit, ii = j // 4, j % 4
+            if j + 1 < 32:
+                t8(j + 1)
             if unit + 1 < 8:
-                norms(unit + 1)
+                for m in pieces[ii]:
+                    stage_a(unit + 1, m)
+            if j + 1 < 32:
+                sq(j + 1)
+            rot(j)
+            if j == 1:
+                front_x(2)
+            if j == 5:
+                front_x(3)
+            if j == 7:
+                load_ftab(2)
+            if j == 15:
+                load_ftab(3)

@@ -42,10 +42,11 @@ def tile_causalwanselfattention_pa_kernel(
         work = ctx.enter_context(tc.tile_pool(name="work", bufs=2))
         stats = ctx.enter_context(tc.tile_pool(name="stats", bufs=4))
         ps = ctx.enter_context(tc.psum_pool(name="ps", bufs=2))
+        ctx.enter_context(tc.manual_schedule(engines={mybir.EngineType.PE, mybir.EngineType.Activation}))
 
         raw = const.tile([P, P], BF16)
         nc.vector.memset(raw[:], 0.0)
-        bz = const.tile([P, 2 * KDIM], BF16)
+        bz = work.tile([P, 2 * KDIM], BF16, tag="o", bufs=3, name="bz")
         nc.vector.memset(bz[:], 0.0)
         sgn = const.tile([P, 2], F32)
         nc.vector.memset(sgn[:, 0:1], 1.0)
@@ -85,14 +86,15 @@ def tile_causalwanselfattention_pa_kernel(
             wraw[j] = wr
 
         gbc = const.tile([P, 2, KDIM], BF16)
+        load_w(0)
         load_x(0)
         sc_bc = const.tile([P, KDIM], F32)
         nc.sync.dma_start(out=sc_bc[:], in_=x_scale.rearrange("o k -> (o k)").partition_broadcast(P))
         nc.sync.dma_start(out=gbc[:, 0, :], in_=gq.partition_broadcast(P))
-        for j in range(4):
+        for j in range(1, 4):
             load_w(j)
-        nc.sync.dma_start(out=gbc[:, 1, :], in_=gk.partition_broadcast(P))
         load_x(1)
+        nc.sync.dma_start(out=gbc[:, 1, :], in_=gk.partition_broadcast(P))
 
         xc = keep.tile([P, NCHUNK, 2, CHUNK], U32, align_bytes=64)
         xs = keep.tile([P, NCHUNK, 2, CHUNK], U8, align_bytes=64)
@@ -107,31 +109,39 @@ def tile_causalwanselfattention_pa_kernel(
                     nc.tensor.transpose(ft[:, 2 * g + u, :], words[:, 256 * g + u:256 * (g + 1):2], identf[:])
             return ft[:].rearrange("p (g u) r -> p g r u", u=2)
 
-        def front_x(c):
-            xg = stage.tile([P, 2, CHUNK, 4], BF16, tag="xg", bufs=2, align_bytes=64, name="xg")
-            for i in range(4):
-                xw = stage.tile([P, KDIM], BF16, tag="xw", bufs=3, name="xw")
-                nc.vector.tensor_tensor(out=xw[:], in0=xb[c][:, i, :].bitcast(FP8), in1=sc_bc[:], op=ALU.mult)
-                ftv = turn(xw[:])
-                nc.scalar.copy(out=xg[:].bitcast(F32)[:, :, P * i:P * (i + 1), :], in_=ftv)
+        xgs = {}
+
+        def front_x_tile(c, i):
+            if i == 0:
+                xgs[c] = stage.tile([P, 2, CHUNK, 4], BF16, tag="xg", bufs=2, align_bytes=64, name="xg")
+            xw = stage.tile([P, KDIM], BF16, tag="xw", bufs=3, name="xw")
+            nc.vector.tensor_tensor(out=xw[:], in0=xb[c][:, i, :].bitcast(FP8), in1=sc_bc[:], op=ALU.mult)
+            ftv = turn(xw[:])
+            nc.scalar.copy(out=xgs[c][:].bitcast(F32)[:, :, P * i:P * (i + 1), :], in_=ftv)
+
+        def front_x_quant(c):
             nc.vector.quantize_mx(
                 out=xc[:, c].rearrange("p g n -> p (g n)").bitcast(FP8X4),
                 scales=xs[:, c].rearrange("p g n -> p (g n)"),
-                in_=xg[:].rearrange("p g r t -> p (g r t)"),
+                in_=xgs[c][:].rearrange("p g r t -> p (g r t)"),
             )
 
-        def front_w(qk):
-            wg = stage.tile([P, 2, KDIM, 4], BF16, tag="wg", bufs=1, align_bytes=64, name="wg")
-            wgw = wg[:].bitcast(F32)
-            for h in range(NH):
-                ftv = turn(wraw[4 * qk + h // 2][:, h % 2, :])
-                nc.scalar.copy(out=wgw[:, :, FR * h:FR * (h + 1), :], in_=ftv[:, :, 0:FR, :])
-                nc.scalar.copy(out=wgw[:, :, FW + HR * h:FW + HR * (h + 1), :], in_=ftv[:, :, FR:P, :])
+        wgs = {}
+
+        def front_w_head(qk, h):
+            if h == 0:
+                wgs[qk] = stage.tile([P, 2, KDIM, 4], BF16, tag="wg", bufs=1, align_bytes=64, name="wg")
+            wgw = wgs[qk][:].bitcast(F32)
+            ftv = turn(wraw[4 * qk + h // 2][:, h % 2, :])
+            nc.scalar.copy(out=wgw[:, :, FR * h:FR * (h + 1), :], in_=ftv[:, :, 0:FR, :])
+            nc.vector.tensor_copy(out=wgw[:, :, FW + HR * h:FW + HR * (h + 1), :], in_=ftv[:, :, FR:P, :])
+
+        def front_w_quant(qk):
             for g in range(2):
                 nc.vector.quantize_mx(
                     out=wc[:, qk, g, :].bitcast(FP8X4),
                     scales=ws[:, qk, g, :],
-                    in_=wg[:, g].rearrange("p r t -> p (r t)"),
+                    in_=wgs[qk][:, g].rearrange("p r t -> p (r t)"),
                 )
 
         ftx = const.tile([P, 2, 64, 2], BF16)
@@ -148,8 +158,6 @@ def tile_causalwanselfattention_pa_kernel(
                 in1=identb[:, 64:80].unsqueeze(1).to_broadcast([P, 8, 16]), op=ALU.add,
             )
             base.append(bs)
-
-        front_x(0)
 
         pt = ps.tile([P, 2, 256], F32, tag="acc", bufs=2, name="pt")
         for hh in range(2):
@@ -168,57 +176,72 @@ def tile_causalwanselfattention_pa_kernel(
         bcol = const.tile([P, 16], F32)
         nc.vector.tensor_copy(out=bcol[:], in_=pb[:])
 
-        rf = const.tile([16, 2, 2 * FW], F32)
+        front_w_head(0, 0)
+        front_w_head(0, 1)
+        front_x_tile(0, 0)
+        front_x_tile(0, 1)
+        front_w_head(0, 2)
+        front_w_head(0, 3)
+        front_x_tile(0, 2)
+        front_x_tile(0, 3)
+        front_x_quant(0)
+        for h in range(4, NH):
+            front_w_head(0, h)
+        front_w_quant(0)
+
         hwtab = const.tile([P, 2, 2, 2, HWW], F32)
         gv = gbc[:].rearrange("p q (h r) -> p q h r", r=P)
 
         def make_rf(qk):
+            rf = work.tile([16, 2 * FW], F32, tag="o", bufs=3, name="rf")
             nc.gpsimd.tensor_tensor(
-                out=rf[:, qk, :].rearrange("p (a h r) -> p a h r", a=2, r=FR),
+                out=rf[:].rearrange("p (a h r) -> p a h r", a=2, r=FR),
                 in0=gv[0:16, qk, :, 0:FR].unsqueeze(1).to_broadcast([16, 2, NH, FR]),
                 in1=ftx[0:16].rearrange("p a c e -> p a (c e)")[:, :, 0:FR].unsqueeze(2).to_broadcast([16, 2, NH, FR]),
                 op=ALU.mult,
             )
-            nc.sync.dma_start(out=outs[1][SCR + 16 * qk:SCR + 16 * qk + 16, 0:2 * FW], in_=rf[:, qk, :])
+            nc.sync.dma_start(out=outs[1][SCR + 16 * qk:SCR + 16 * qk + 16, 0:2 * FW], in_=rf[:])
 
-        def make_hw(qk, hh):
+        def make_hw(qk, hh, a):
             nc.gpsimd.tensor_tensor(
-                out=hwtab[:, qk, hh].rearrange("p a (h r) -> p a h r", r=HR),
-                in0=gv[:, qk, :, FR:P].unsqueeze(1).to_broadcast([P, 2, NH, HR]),
-                in1=tabs[:, hh, :, FR:P].unsqueeze(2).to_broadcast([P, 2, NH, HR]),
+                out=hwtab[:, qk, hh, a].rearrange("p (h r) -> p h r", r=HR),
+                in0=gv[:, qk, :, FR:P],
+                in1=tabs[:, hh, a, FR:P].unsqueeze(1).to_broadcast([P, NH, HR]),
                 op=ALU.mult,
             )
 
         ftab = {}
 
-        def load_ftab(c):
-            ft_c = work.tile([P, 2, 2, 2, FW], F32, tag="ftab", bufs=2, name="ftab")
-            for qk in range(2):
-                for f2 in range(2):
-                    nc.sync.dma_start(
-                        out=ft_c[:, f2, qk].rearrange("p a x -> p (a x)"),
-                        in_=outs[1][SCR + 16 * qk + 2 * c + f2:SCR + 16 * qk + 2 * c + f2 + 1, 0:2 * FW]
-                        .rearrange("o x -> (o x)").partition_broadcast(P),
-                    )
-            ftab[c] = ft_c
+        def load_ftab(c, qk):
+            if qk == 0:
+                ftab[c] = work.tile([P, 2, 2, 2, FW], F32, tag="ftab", bufs=2, name="ftab")
+            for f2 in range(2):
+                row = SCR + 16 * qk + 2 * c + f2
+                nc.sync.dma_start(
+                    out=ftab[c][:, f2, qk].rearrange("p a x -> p (a x)"),
+                    in_=outs[1][row:row + 1, 0:2 * FW].rearrange("o x -> (o x)").partition_broadcast(P),
+                )
 
         make_rf(0)
-        make_hw(0, 0)
-        make_hw(0, 1)
+        load_ftab(0, 0)
+        load_ftab(1, 0)
+        for hh in range(2):
+            for a in range(2):
+                make_hw(0, hh, a)
         make_rf(1)
-        make_hw(1, 0)
-        make_hw(1, 1)
-
-        front_w(0)
+        load_ftab(0, 1)
+        load_ftab(1, 1)
         for j in range(4, 8):
             load_w(j)
-        load_ftab(0)
         load_x(2)
+
+        units = ((0, 0), (1, 0), (0, 1), (1, 1), (2, 0), (2, 1), (3, 0), (3, 1))
 
         yT = {}
 
-        def stage_a(unit, m):
-            c, qk = unit // 2, unit % 2
+        def stage_a(a):
+            unit, m = a // 8, a % 8
+            c, qk = units[unit]
             acc = ps.tile([P, CHUNK], F32, tag="acc", bufs=2, name="acc")
             for g in range(2):
                 nc.tensor.matmul_mx(
@@ -230,7 +253,7 @@ def tile_causalwanselfattention_pa_kernel(
                     start=(g == 0),
                     stop=(g == 1),
                 )
-            yt = ypool.tile([P, CHUNK], F32, tag="yT%d" % m, bufs=2, name="yT%d" % m)
+            yt = ypool.tile([P, CHUNK], F32, tag="yT", bufs=20, name="yT")
             nc.scalar.activation(
                 out=yt[:], in_=acc[:], func=ACT.Identity, bias=bcol[:, 8 * qk + m:8 * qk + m + 1], scale=1.0
             )
@@ -239,38 +262,41 @@ def tile_causalwanselfattention_pa_kernel(
         yn = {}
         rstd = {}
 
-        def t8(j):
+        def t4(j, b):
             unit, ii = j // 4, j % 4
-            banks = []
-            for b in range(2):
-                y = ps.tile([P, 4, P], F32, tag="yn", bufs=6, name="yn")
-                for mm in range(4):
-                    nc.tensor.transpose(y[:, mm, :], yT[(unit, 4 * b + mm)][:, P * ii:P * (ii + 1)], identf[:])
-                banks.append(y)
-            yn[j] = banks
+            y = ps.tile([P, 4, P], F32, tag="yn", bufs=6, name="yn")
+            for mm in range(4):
+                nc.tensor.transpose(y[:, mm, :], yT[(unit, 4 * b + mm)][:, P * ii:P * (ii + 1)], identf[:])
+            yn[(j, b)] = y
 
-        def sq(j):
-            s2 = stats.tile([P, 2], F32, name="s2")
-            for b in range(2):
-                junk = work.tile([P, CHUNK], BF16, tag="junk", bufs=2, name="junk")
-                nc.scalar.activation(
-                    out=junk[:], in_=yn[j][b][:].rearrange("p m r -> p (m r)"), func=ACT.Square,
-                    scale=1.0 / 32.0, accum_out=s2[:, b:b + 1],
-                )
+        sums = {}
+
+        def sq_bank(j, b):
+            if b == 0:
+                sums[j] = stats.tile([P, 2], F32, name="s2")
+            junk = work.tile([P, CHUNK], BF16, tag="junk", bufs=2, name="junk")
+            nc.scalar.activation(
+                out=junk[:], in_=yn[(j, b)][:].rearrange("p m r -> p (m r)"), func=ACT.Square,
+                scale=1.0 / 32.0, accum_out=sums[j][:, b:b + 1],
+            )
+
+        def sq_fin(j):
             j2 = stats.tile([P, 2], F32, name="j2")
             ms = stats.tile([P, 1], F32, name="ms")
-            nc.scalar.activation(out=j2[:], in_=s2[:], func=ACT.Identity, bias=0.5 * EPS, scale=1.0, accum_out=ms[:])
+            nc.scalar.activation(
+                out=j2[:], in_=sums[j][:], func=ACT.Identity, bias=0.5 * EPS, scale=1.0, accum_out=ms[:]
+            )
             rs = stats.tile([P, 1], F32, name="rs")
             nc.scalar.activation(out=rs[:], in_=ms[:], func=ACT.Abs_reciprocal_sqrt)
             rstd[j] = rs
 
         def rot(j):
             unit, ii = j // 4, j % 4
-            c, qk = unit // 2, unit % 2
+            c, qk = units[unit]
             f2, hh = ii // 2, ii % 2
             i = 4 * c + ii
-            y0 = yn[j][0][:].rearrange("p m r -> p (m r)")
-            y1 = yn[j][1][:].rearrange("p m r -> p (m r)")
+            y0 = yn[(j, 0)][:].rearrange("p m r -> p (m r)")
+            y1 = yn[(j, 1)][:].rearrange("p m r -> p (m r)")
             uv = work.tile([P, 2, KDIM], F32, tag="uv", bufs=2, name="uv")
             for src, lo, hi, tabv in (
                 (y0[:, 0:FW], 0, FW, ftab[c][:, f2, qk]),
@@ -291,31 +317,54 @@ def tile_causalwanselfattention_pa_kernel(
                 )
             nc.sync.dma_start(out=outs[qk][P * i:P * (i + 1), :], in_=o[:].rearrange("p h r -> p (h r)"))
 
-        for m in range(8):
-            stage_a(0, m)
-        front_w(1)
-        front_x(1)
+        for i in range(4):
+            stage_a(2 * i)
+            stage_a(2 * i + 1)
+            front_x_tile(1, i)
+        front_x_quant(1)
         load_x(3)
-        load_ftab(1)
-        t8(0)
-        sq(0)
+        for b in range(2):
+            t4(0, b)
+            sq_bank(0, b)
+        sq_fin(0)
 
-        pieces = ((0, 1, 2), (3, 4, 5), (6, 7), ())
+        later = {}
+
+        def at(j, fn, *args):
+            later.setdefault(j, []).append((fn, args))
+
+        for h in range(NH):
+            at(h // 3, front_w_head, 1, h)
+        at(2, front_w_quant, 1)
+        for n in range(4):
+            at(n, make_hw, 1, n // 2, n % 2)
+        for i in range(4):
+            at(5 + i, front_x_tile, 2, i)
+            at(13 + i, front_x_tile, 3, i)
+        at(9, front_x_quant, 2)
+        at(17, front_x_quant, 3)
+        at(11, load_ftab, 2, 0)
+        at(11, load_ftab, 2, 1)
+        at(15, load_ftab, 3, 0)
+        at(15, load_ftab, 3, 1)
+
+        nxt = 8
         for j in range(32):
-            unit, ii = j // 4, j % 4
+            todo = []
+            while nxt < 64 and nxt < 2 * j + 12 and len(todo) < 3:
+                todo.append(nxt)
+                nxt += 1
+            for b in range(2):
+                if j + 1 < 32:
+                    t4(j + 1, b)
+                if b < len(todo):
+                    stage_a(todo[b])
+                if j + 1 < 32:
+                    sq_bank(j + 1, b)
+            for a in todo[2:]:
+                stage_a(a)
             if j + 1 < 32:
-                t8(j + 1)
-            if unit + 1 < 8:
-                for m in pieces[ii]:
-                    stage_a(unit + 1, m)
-            if j + 1 < 32:
-                sq(j + 1)
+                sq_fin(j + 1)
             rot(j)
-            if j == 1:
-                front_x(2)
-            if j == 5:
-                front_x(3)
-            if j == 7:
-                load_ftab(2)
-            if j == 15:
-                load_ftab(3)
+            for fn, args in later.get(j, ()):
+                fn(*args)

@@ -42,7 +42,7 @@ def tile_causalwanselfattention_pa_kernel(
         work = ctx.enter_context(tc.tile_pool(name="work", bufs=2))
         stats = ctx.enter_context(tc.tile_pool(name="stats", bufs=4))
         ps = ctx.enter_context(tc.psum_pool(name="ps", bufs=2))
-        ctx.enter_context(tc.manual_schedule(engines={mybir.EngineType.PE, mybir.EngineType.Activation}))
+        ctx.enter_context(tc.manual_schedule(engines={mybir.EngineType.PE, mybir.EngineType.Activation, mybir.EngineType.SP}))
 
         raw = const.tile([P, P], BF16)
         nc.vector.memset(raw[:], 0.0)
@@ -90,9 +90,9 @@ def tile_causalwanselfattention_pa_kernel(
         load_x(0)
         sc_bc = const.tile([P, KDIM], F32)
         nc.sync.dma_start(out=sc_bc[:], in_=x_scale.rearrange("o k -> (o k)").partition_broadcast(P))
-        nc.sync.dma_start(out=gbc[:, 0, :], in_=gq.partition_broadcast(P))
         for j in range(1, 4):
             load_w(j)
+        nc.sync.dma_start(out=gbc[:, 0, :], in_=gq.partition_broadcast(P))
         load_x(1)
         nc.sync.dma_start(out=gbc[:, 1, :], in_=gk.partition_broadcast(P))
 
@@ -103,7 +103,7 @@ def tile_causalwanselfattention_pa_kernel(
 
         def turn(rows_bf16):
             words = rows_bf16.bitcast(F32)
-            ft = ps.tile([P, 4, P], F32, tag="acc", bufs=2, name="ft")
+            ft = ps.tile([P, 4, P], F32, tag="yn", bufs=6, name="ft")
             for g in range(2):
                 for u in range(2):
                     nc.tensor.transpose(ft[:, 2 * g + u, :], words[:, 256 * g + u:256 * (g + 1):2], identf[:])
@@ -134,7 +134,7 @@ def tile_causalwanselfattention_pa_kernel(
             wgw = wgs[qk][:].bitcast(F32)
             ftv = turn(wraw[4 * qk + h // 2][:, h % 2, :])
             nc.scalar.copy(out=wgw[:, :, FR * h:FR * (h + 1), :], in_=ftv[:, :, 0:FR, :])
-            nc.vector.tensor_copy(out=wgw[:, :, FW + HR * h:FW + HR * (h + 1), :], in_=ftv[:, :, FR:P, :])
+            nc.scalar.copy(out=wgw[:, :, FW + HR * h:FW + HR * (h + 1), :], in_=ftv[:, :, FR:P, :])
 
         def front_w_quant(qk):
             for g in range(2):
@@ -159,37 +159,8 @@ def tile_causalwanselfattention_pa_kernel(
             )
             base.append(bs)
 
-        pt = ps.tile([P, 2, 256], F32, tag="acc", bufs=2, name="pt")
-        for hh in range(2):
-            nc.tensor.matmul(
-                out=pt[:, hh, :], lhsT=base[hh][:].rearrange("k a b -> k (a b)"),
-                rhs=ftx[:].rearrange("k a c e -> k (a c e)"), start=True, stop=True,
-            )
-        tabs = const.tile([P, 2, 2, P], BF16)
-        nc.scalar.copy(out=tabs[:].rearrange("p s a r -> p s (a r)"), in_=pt[:])
-
-        pb = ps.tile([P, 16], F32, tag="acc", bufs=2, name="pb")
-        for idx in range(16):
-            nc.tensor.matmul(
-                out=pb[:, idx:idx + 1], lhsT=bz[:, P * idx:P * (idx + 1)], rhs=identb[:, 0:1], start=True, stop=True
-            )
-        bcol = const.tile([P, 16], F32)
-        nc.vector.tensor_copy(out=bcol[:], in_=pb[:])
-
-        front_w_head(0, 0)
-        front_w_head(0, 1)
-        front_x_tile(0, 0)
-        front_x_tile(0, 1)
-        front_w_head(0, 2)
-        front_w_head(0, 3)
-        front_x_tile(0, 2)
-        front_x_tile(0, 3)
-        front_x_quant(0)
-        for h in range(4, NH):
-            front_w_head(0, h)
-        front_w_quant(0)
-
         hwtab = const.tile([P, 2, 2, 2, HWW], F32)
+        tabs = const.tile([P, 2, 2, P], BF16)
         gv = gbc[:].rearrange("p q (h r) -> p q h r", r=P)
 
         def make_rf(qk):
@@ -222,18 +193,53 @@ def tile_causalwanselfattention_pa_kernel(
                     in_=outs[1][row:row + 1, 0:2 * FW].rearrange("o x -> (o x)").partition_broadcast(P),
                 )
 
+        front_w_head(0, 0)
+        front_w_head(0, 1)
+        load_w(4)
+        front_x_tile(0, 0)
+        front_x_tile(0, 1)
+        pt = ps.tile([P, 2, 256], F32, tag="acc", bufs=2, name="pt")
+        for hh in range(2):
+            nc.tensor.matmul(
+                out=pt[:, hh, :], lhsT=base[hh][:].rearrange("k a b -> k (a b)"),
+                rhs=ftx[:].rearrange("k a c e -> k (a c e)"), start=True, stop=True,
+            )
+        nc.scalar.copy(out=tabs[:].rearrange("p s a r -> p s (a r)"), in_=pt[:])
+        front_x_tile(0, 2)
+        front_x_tile(0, 3)
+        front_x_quant(0)
+        load_x(2)
+        front_w_head(0, 2)
+        front_w_head(0, 3)
+        load_w(5)
         make_rf(0)
         load_ftab(0, 0)
-        load_ftab(1, 0)
-        for hh in range(2):
-            for a in range(2):
-                make_hw(0, hh, a)
+        front_w_head(0, 4)
+        front_w_head(0, 5)
+        load_w(6)
+        pb = ps.tile([P, 16], F32, tag="acc", bufs=2, name="pb")
+        for idx in range(16):
+            nc.tensor.matmul(
+                out=pb[:, idx:idx + 1], lhsT=bz[:, P * idx:P * (idx + 1)], rhs=identb[:, 0:1], start=True, stop=True
+            )
+        bcol = const.tile([P, 16], F32)
+        nc.vector.tensor_copy(out=bcol[:], in_=pb[:])
+        front_w_head(0, 6)
+        front_w_head(0, 7)
+        load_w(7)
+        front_w_quant(0)
         make_rf(1)
+        for i in range(4):
+            front_x_tile(1, i)
+        front_x_quant(1)
+        load_x(3)
+        load_ftab(1, 0)
         load_ftab(0, 1)
         load_ftab(1, 1)
-        for j in range(4, 8):
-            load_w(j)
-        load_x(2)
+        for qk in range(2):
+            for hh in range(2):
+                for a in range(2):
+                    make_hw(qk, hh, a)
 
         units = ((0, 0), (1, 0), (0, 1), (1, 1), (2, 0), (2, 1), (3, 0), (3, 1))
 
@@ -320,9 +326,13 @@ def tile_causalwanselfattention_pa_kernel(
         for i in range(4):
             stage_a(2 * i)
             stage_a(2 * i + 1)
-            front_x_tile(1, i)
-        front_x_quant(1)
-        load_x(3)
+            front_w_head(1, 2 * i)
+            front_w_head(1, 2 * i + 1)
+        front_w_quant(1)
+        for c in (2, 3):
+            for i in range(4):
+                front_x_tile(c, i)
+            front_x_quant(c)
         for b in range(2):
             t4(0, b)
             sq_bank(0, b)
@@ -333,16 +343,6 @@ def tile_causalwanselfattention_pa_kernel(
         def at(j, fn, *args):
             later.setdefault(j, []).append((fn, args))
 
-        for h in range(NH):
-            at(h // 3, front_w_head, 1, h)
-        at(2, front_w_quant, 1)
-        for n in range(4):
-            at(n, make_hw, 1, n // 2, n % 2)
-        for i in range(4):
-            at(5 + i, front_x_tile, 2, i)
-            at(13 + i, front_x_tile, 3, i)
-        at(9, front_x_quant, 2)
-        at(17, front_x_quant, 3)
         at(11, load_ftab, 2, 0)
         at(11, load_ftab, 2, 1)
         at(15, load_ftab, 3, 0)

@@ -51,28 +51,21 @@ def tile_causalwanselfattention_pa_kernel(
         sgn = const.tile([P, 2], F32)
         nc.vector.memset(sgn[:, 0:1], 1.0)
         nc.vector.memset(sgn[:, 1:2], -1.0)
+        warm = const.tile([P, 1], F32)
+        nc.scalar.activation(out=warm[:], in_=sgn[:, 0:1], func=ACT.Abs_reciprocal_sqrt)
+        for half, tabl in enumerate((freqs_cos, freqs_sin)):
+            for r0, c0, c1 in ((0, 0, 22), (32, 22, 43), (64, 43, 64)):
+                nc.scalar.dma_start(out=raw[r0:r0 + 16, 64 * half + c0:64 * half + c1], in_=tabl[:, c0:c1])
         identf = const.tile([P, P], F32)
         make_identity(nc, identf[:])
         identb = const.tile([P, P], BF16)
         make_identity(nc, identb[:])
 
-        for half, tabl in enumerate((freqs_cos, freqs_sin)):
-            for r0, c0, c1 in ((0, 0, 22), (32, 22, 43), (64, 43, 64)):
-                nc.scalar.dma_start(out=raw[r0:r0 + 16, 64 * half + c0:64 * half + c1], in_=tabl[:, c0:c1])
-        for qk, vec in enumerate((bq, bk)):
-            v3 = vec.rearrange("(o h r) -> o h r", o=1, r=P)
-            nc.scalar.dma_start(
-                out=bz[0:1, KDIM * qk:KDIM * qk + FW].rearrange("o (h r) -> o h r", r=FR), in_=v3[:, :, 0:FR]
-            )
-            nc.scalar.dma_start(
-                out=bz[0:1, KDIM * qk + FW:KDIM * (qk + 1)].rearrange("o (h r) -> o h r", r=HR), in_=v3[:, :, FR:P]
-            )
-
         xb = {}
         wraw = {}
 
         def load_x(c):
-            xb_c = stage.tile([P, 4, KDIM], U8, tag="xb", bufs=2, name="xb")
+            xb_c = stage.tile([P, 4, KDIM], U8, tag="xb", bufs=4, name="xb")
             nc.sync.dma_start(
                 out=xb_c[:], in_=x_bytes[CHUNK * c:CHUNK * (c + 1), :].rearrange("(i p) k -> p i k", p=P)
             )
@@ -92,9 +85,15 @@ def tile_causalwanselfattention_pa_kernel(
         nc.sync.dma_start(out=sc_bc[:], in_=x_scale.rearrange("o k -> (o k)").partition_broadcast(P))
         for j in range(1, 4):
             load_w(j)
-        nc.sync.dma_start(out=gbc[:, 0, :], in_=gq.partition_broadcast(P))
+        for qk, vec in enumerate((bq, bk)):
+            v3 = vec.rearrange("(o h r) -> o h r", o=1, r=P)
+            nc.sync.dma_start(
+                out=bz[0:1, KDIM * qk:KDIM * qk + FW].rearrange("o (h r) -> o h r", r=FR), in_=v3[:, :, 0:FR]
+            )
+            nc.sync.dma_start(
+                out=bz[0:1, KDIM * qk + FW:KDIM * (qk + 1)].rearrange("o (h r) -> o h r", r=HR), in_=v3[:, :, FR:P]
+            )
         load_x(1)
-        nc.sync.dma_start(out=gbc[:, 1, :], in_=gk.partition_broadcast(P))
 
         xc = keep.tile([P, NCHUNK, 2, CHUNK], U32, align_bytes=64)
         xs = keep.tile([P, NCHUNK, 2, CHUNK], U8, align_bytes=64)
@@ -165,7 +164,7 @@ def tile_causalwanselfattention_pa_kernel(
 
         def make_rf(qk):
             rf = work.tile([16, 2 * FW], F32, tag="o", bufs=3, name="rf")
-            nc.gpsimd.tensor_tensor(
+            nc.vector.tensor_tensor(
                 out=rf[:].rearrange("p (a h r) -> p a h r", a=2, r=FR),
                 in0=gv[0:16, qk, :, 0:FR].unsqueeze(1).to_broadcast([16, 2, NH, FR]),
                 in1=ftx[0:16].rearrange("p a c e -> p a (c e)")[:, :, 0:FR].unsqueeze(2).to_broadcast([16, 2, NH, FR]),
@@ -174,7 +173,7 @@ def tile_causalwanselfattention_pa_kernel(
             nc.sync.dma_start(out=outs[1][SCR + 16 * qk:SCR + 16 * qk + 16, 0:2 * FW], in_=rf[:])
 
         def make_hw(qk, hh, a):
-            nc.gpsimd.tensor_tensor(
+            nc.vector.tensor_tensor(
                 out=hwtab[:, qk, hh, a].rearrange("p (h r) -> p h r", r=HR),
                 in0=gv[:, qk, :, FR:P],
                 in1=tabs[:, hh, a, FR:P].unsqueeze(1).to_broadcast([P, NH, HR]),
@@ -196,6 +195,7 @@ def tile_causalwanselfattention_pa_kernel(
         front_w_head(0, 0)
         front_w_head(0, 1)
         load_w(4)
+        load_x(2)
         front_x_tile(0, 0)
         front_x_tile(0, 1)
         pt = ps.tile([P, 2, 256], F32, tag="acc", bufs=2, name="pt")
@@ -208,12 +208,10 @@ def tile_causalwanselfattention_pa_kernel(
         front_x_tile(0, 2)
         front_x_tile(0, 3)
         front_x_quant(0)
-        load_x(2)
         front_w_head(0, 2)
         front_w_head(0, 3)
         load_w(5)
-        make_rf(0)
-        load_ftab(0, 0)
+        load_x(3)
         front_w_head(0, 4)
         front_w_head(0, 5)
         load_w(6)
@@ -227,13 +225,16 @@ def tile_causalwanselfattention_pa_kernel(
         front_w_head(0, 6)
         front_w_head(0, 7)
         load_w(7)
+        nc.sync.dma_start(out=gbc[:, 0, :], in_=gq.partition_broadcast(P))
+        nc.sync.dma_start(out=gbc[:, 1, :], in_=gk.partition_broadcast(P))
         front_w_quant(0)
-        make_rf(1)
         for i in range(4):
             front_x_tile(1, i)
         front_x_quant(1)
-        load_x(3)
+        make_rf(0)
+        load_ftab(0, 0)
         load_ftab(1, 0)
+        make_rf(1)
         load_ftab(0, 1)
         load_ftab(1, 1)
         for qk in range(2):
@@ -259,7 +260,7 @@ def tile_causalwanselfattention_pa_kernel(
                     start=(g == 0),
                     stop=(g == 1),
                 )
-            yt = ypool.tile([P, CHUNK], F32, tag="yT", bufs=20, name="yT")
+            yt = ypool.tile([P, CHUNK], F32, tag="yT", bufs=16, name="yT")
             nc.scalar.activation(
                 out=yt[:], in_=acc[:], func=ACT.Identity, bias=bcol[:, 8 * qk + m:8 * qk + m + 1], scale=1.0
             )

@@ -287,14 +287,19 @@ def tile_causalwanselfattention_pa_kernel(
                 scale=1.0 / 32.0, accum_out=sums[j][:, b:b + 1],
             )
 
-        def sq_fin(j):
+        means = {}
+
+        def sq_sum(j):
             j2 = stats.tile([P, 2], F32, name="j2")
             ms = stats.tile([P, 1], F32, name="ms")
             nc.scalar.activation(
                 out=j2[:], in_=sums[j][:], func=ACT.Identity, bias=0.5 * EPS, scale=1.0, accum_out=ms[:]
             )
+            means[j] = ms
+
+        def sq_root(j):
             rs = stats.tile([P, 1], F32, name="rs")
-            nc.scalar.activation(out=rs[:], in_=ms[:], func=ACT.Abs_reciprocal_sqrt)
+            nc.scalar.activation(out=rs[:], in_=means[j][:], func=ACT.Abs_reciprocal_sqrt)
             rstd[j] = rs
 
         def rot(j):
@@ -337,7 +342,8 @@ def tile_causalwanselfattention_pa_kernel(
         for b in range(2):
             t4(0, b)
             sq_bank(0, b)
-        sq_fin(0)
+        sq_sum(0)
+        sq_root(0)
 
         later = {}
 
@@ -355,17 +361,18 @@ def tile_causalwanselfattention_pa_kernel(
             while nxt < 64 and nxt < 2 * j + 12 and len(todo) < 3:
                 todo.append(nxt)
                 nxt += 1
-            for b in range(2):
-                if j + 1 < 32:
+            if j + 1 < 32:
+                for b in range(2):
                     t4(j + 1, b)
-                if b < len(todo):
-                    stage_a(todo[b])
-                if j + 1 < 32:
                     sq_bank(j + 1, b)
-            for a in todo[2:]:
+            for a in todo[0:1]:
                 stage_a(a)
             if j + 1 < 32:
-                sq_fin(j + 1)
+                sq_sum(j + 1)
+            for a in todo[1:]:
+                stage_a(a)
+            if j + 1 < 32:
+                sq_root(j + 1)
             rot(j)
             for fn, args in later.get(j, ()):
                 fn(*args)

@@ -81,8 +81,8 @@ def tile_causalwanselfattention_pa_kernel(
         gbc = const.tile([P, 2, KDIM], BF16)
         load_w(0)
         load_x(0)
-        sc_bc = const.tile([P, KDIM], F32)
-        nc.sync.dma_start(out=sc_bc[:], in_=x_scale.rearrange("o k -> (o k)").partition_broadcast(P))
+        sc_t = const.tile([P, 2, 4], F32)
+        nc.sync.dma_start(out=sc_t[:], in_=x_scale.rearrange("o (g p t) -> p (o g) t", p=P, t=4))
         for j in range(1, 4):
             load_w(j)
         for qk, vec in enumerate((bq, bk)):
@@ -101,12 +101,15 @@ def tile_causalwanselfattention_pa_kernel(
         ws = keep.tile([P, 2, 2, KDIM], U8, align_bytes=64)
 
         def turn(rows_bf16):
+            return turn_raw(rows_bf16)[:].rearrange("p (g u) r -> p g r u", u=2)
+
+        def turn_raw(rows_bf16):
             words = rows_bf16.bitcast(F32)
             ft = ps.tile([P, 4, P], F32, tag="yn", bufs=6, name="ft")
             for g in range(2):
                 for u in range(2):
                     nc.tensor.transpose(ft[:, 2 * g + u, :], words[:, 256 * g + u:256 * (g + 1):2], identf[:])
-            return ft[:].rearrange("p (g u) r -> p g r u", u=2)
+            return ft
 
         xgs = {}
 
@@ -114,9 +117,18 @@ def tile_causalwanselfattention_pa_kernel(
             if i == 0:
                 xgs[c] = stage.tile([P, 2, CHUNK, 4], BF16, tag="xg", bufs=2, align_bytes=64, name="xg")
             xw = stage.tile([P, KDIM], BF16, tag="xw", bufs=3, name="xw")
-            nc.vector.tensor_tensor(out=xw[:], in0=xb[c][:, i, :].bitcast(FP8), in1=sc_bc[:], op=ALU.mult)
-            ftv = turn(xw[:])
-            nc.scalar.copy(out=xgs[c][:].bitcast(F32)[:, :, P * i:P * (i + 1), :], in_=ftv)
+            nc.scalar.copy(out=xw[:], in_=xb[c][:, i, :].bitcast(FP8))
+            ft = turn_raw(xw[:])
+            halves = ft[:].rearrange("p a r -> p (a r)").bitcast(BF16).rearrange(
+                "p (g u r e) -> p g r u e", g=2, u=2, e=2
+            )
+            for g in range(2):
+                nc.vector.tensor_tensor(
+                    out=xgs[c][:, g, P * i:P * (i + 1), :].rearrange("p r (u e) -> p r u e", e=2),
+                    in0=halves[:, g],
+                    in1=sc_t[:, g, :].rearrange("p (u e) -> p u e", e=2).unsqueeze(1).to_broadcast([P, P, 2, 2]),
+                    op=ALU.mult,
+                )
 
         def front_x_quant(c):
             nc.vector.quantize_mx(

@@ -53,9 +53,6 @@ def tile_causalwanselfattention_pa_kernel(
         nc.vector.memset(sgn[:, 1:2], -1.0)
         warm = const.tile([P, 1], F32)
         nc.scalar.activation(out=warm[:], in_=sgn[:, 0:1], func=ACT.Abs_reciprocal_sqrt)
-        for half, tabl in enumerate((freqs_cos, freqs_sin)):
-            for r0, c0, c1 in ((0, 0, 22), (32, 22, 43), (64, 43, 64)):
-                nc.scalar.dma_start(out=raw[r0:r0 + 16, 64 * half + c0:64 * half + c1], in_=tabl[:, c0:c1])
         identf = const.tile([P, P], F32)
         make_identity(nc, identf[:])
         identb = const.tile([P, P], BF16)
@@ -83,6 +80,10 @@ def tile_causalwanselfattention_pa_kernel(
         load_x(0)
         sc_t = const.tile([P, 2, 4], F32)
         nc.sync.dma_start(out=sc_t[:], in_=x_scale.rearrange("o (g p t) -> p (o g) t", p=P, t=4))
+        for half, tabl in enumerate((freqs_cos, freqs_sin)):
+            for r0, c0, c1 in ((0, 0, 22), (32, 22, 43), (64, 42, 64)):
+                nc.sync.dma_start(out=raw[r0:r0 + 16, 64 * half + c0:64 * half + c1], in_=tabl[:, c0:c1])
+            nc.vector.memset(raw[64:80, 64 * half + 42:64 * half + 43], 0.0)
         for j in range(1, 4):
             load_w(j)
         for qk, vec in enumerate((bq, bk)):
@@ -101,15 +102,12 @@ def tile_causalwanselfattention_pa_kernel(
         ws = keep.tile([P, 2, 2, KDIM], U8, align_bytes=64)
 
         def turn(rows_bf16):
-            return turn_raw(rows_bf16)[:].rearrange("p (g u) r -> p g r u", u=2)
-
-        def turn_raw(rows_bf16):
             words = rows_bf16.bitcast(F32)
             ft = ps.tile([P, 4, P], F32, tag="yn", bufs=6, name="ft")
             for g in range(2):
                 for u in range(2):
                     nc.tensor.transpose(ft[:, 2 * g + u, :], words[:, 256 * g + u:256 * (g + 1):2], identf[:])
-            return ft
+            return ft[:].rearrange("p (g u) r -> p g r u", u=2)
 
         xgs = {}
 
@@ -118,17 +116,17 @@ def tile_causalwanselfattention_pa_kernel(
                 xgs[c] = stage.tile([P, 2, CHUNK, 4], BF16, tag="xg", bufs=2, align_bytes=64, name="xg")
             xw = stage.tile([P, KDIM], BF16, tag="xw", bufs=3, name="xw")
             nc.scalar.copy(out=xw[:], in_=xb[c][:, i, :].bitcast(FP8))
-            ft = turn_raw(xw[:])
-            halves = ft[:].rearrange("p a r -> p (a r)").bitcast(BF16).rearrange(
-                "p (g u r e) -> p g r u e", g=2, u=2, e=2
-            )
+            words = xw[:].bitcast(F32)
+            ft = ps.tile([P, 2, P, 2], F32, tag="yn", bufs=6, name="fx")
             for g in range(2):
-                nc.vector.tensor_tensor(
-                    out=xgs[c][:, g, P * i:P * (i + 1), :].rearrange("p r (u e) -> p r u e", e=2),
-                    in0=halves[:, g],
-                    in1=sc_t[:, g, :].rearrange("p (u e) -> p u e", e=2).unsqueeze(1).to_broadcast([P, P, 2, 2]),
-                    op=ALU.mult,
-                )
+                for u in range(2):
+                    nc.tensor.transpose(ft[:, g, :, u], words[:, 256 * g + u:256 * (g + 1):2], identf[:])
+            nc.vector.tensor_tensor(
+                out=xgs[c][:, :, P * i:P * (i + 1), :],
+                in0=ft[:].rearrange("p g r u -> p (g r u)").bitcast(BF16).rearrange("p (g r t) -> p g r t", g=2, t=4),
+                in1=sc_t[:].unsqueeze(2).to_broadcast([P, 2, P, 4]),
+                op=ALU.mult,
+            )
 
         def front_x_quant(c):
             nc.vector.quantize_mx(

@@ -114,8 +114,8 @@ def tile_causalwanselfattention_pa_kernel(
         def front_x_tile(c, i):
             if i == 0:
                 xgs[c] = stage.tile([P, 2, CHUNK, 4], BF16, tag="xg", bufs=2, align_bytes=64, name="xg")
-            xw = stage.tile([P, KDIM], BF16, tag="xw", bufs=3, name="xw")
-            nc.scalar.copy(out=xw[:], in_=xb[c][:, i, :].bitcast(FP8))
+            xw = stage.tile([P, KDIM], BF16, tag="xw", bufs=8, name="xw")
+            nc.gpsimd.tensor_copy(out=xw[:], in_=xb[c][:, i, :].bitcast(FP8))
             words = xw[:].bitcast(F32)
             ft = ps.tile([P, 2, P, 2], F32, tag="yn", bufs=6, name="fx")
             for g in range(2):

@@ -46,6 +46,8 @@ def tile_causalwanselfattention_pa_kernel(
 
         raw = const.tile([P, P], BF16)
         nc.vector.memset(raw[:], 0.0)
+        graw = const.tile([P, P], BF16)
+        nc.vector.memset(graw[:], 0.0)
         bz = work.tile([P, 2 * KDIM], BF16, tag="o", bufs=3, name="bz")
         nc.vector.memset(bz[:], 0.0)
         sgn = const.tile([P, 2], F32)
@@ -75,7 +77,6 @@ def tile_causalwanselfattention_pa_kernel(
             nc.sync.dma_start(out=wr[:], in_=w[r0:r0 + 256, :].rearrange("(m p) k -> p m k", p=P))
             wraw[j] = wr
 
-        gbc = const.tile([P, 2, KDIM], BF16)
         load_w(0)
         load_x(0)
         sc_t = const.tile([P, 2, 4], F32)
@@ -84,6 +85,8 @@ def tile_causalwanselfattention_pa_kernel(
             for r0, c0, c1 in ((0, 0, 22), (32, 22, 43), (64, 42, 64)):
                 nc.sync.dma_start(out=raw[r0:r0 + 16, 64 * half + c0:64 * half + c1], in_=tabl[:, c0:c1])
             nc.vector.memset(raw[64:80, 64 * half + 42:64 * half + 43], 0.0)
+        for qk, vec in enumerate((gq, gk)):
+            nc.sync.dma_start(out=graw[NH * qk:NH * (qk + 1), :], in_=vec.rearrange("(h r) -> h r", r=P))
         for j in range(1, 4):
             load_w(j)
         for qk, vec in enumerate((bq, bk)):
@@ -114,7 +117,7 @@ def tile_causalwanselfattention_pa_kernel(
         def front_x_tile(c, i):
             if i == 0:
                 xgs[c] = stage.tile([P, 2, CHUNK, 4], BF16, tag="xg", bufs=2, align_bytes=64, name="xg")
-            xw = stage.tile([P, KDIM], BF16, tag="xw", bufs=8, name="xw")
+            xw = stage.tile([P, KDIM], BF16, tag="xw", bufs=4, name="xw")
             nc.gpsimd.tensor_copy(out=xw[:], in_=xb[c][:, i, :].bitcast(FP8))
             words = xw[:].bitcast(F32)
             ft = ps.tile([P, 2, P, 2], F32, tag="yn", bufs=6, name="fx")
@@ -159,36 +162,60 @@ def tile_causalwanselfattention_pa_kernel(
             out=ftx[:, 1], in0=raw[:, 64:128].unsqueeze(2).to_broadcast([P, 64, 2]),
             in1=sgn[:].unsqueeze(1).to_broadcast([P, 64, 2]), op=ALU.mult,
         )
-        base = []
+        base = const.tile([P, 2, 8, 16], BF16)
         for hh in range(2):
-            bs = const.tile([P, 8, 16], BF16, name="base%d" % hh)
             nc.vector.tensor_tensor(
-                out=bs[:], in0=identb[:, 32 + 8 * hh:40 + 8 * hh].unsqueeze(2).to_broadcast([P, 8, 16]),
+                out=base[:, hh], in0=identb[:, 32 + 8 * hh:40 + 8 * hh].unsqueeze(2).to_broadcast([P, 8, 16]),
                 in1=identb[:, 64:80].unsqueeze(1).to_broadcast([P, 8, 16]), op=ALU.add,
             )
-            base.append(bs)
 
         hwtab = const.tile([P, 2, 2, 2, HWW], F32)
-        tabs = const.tile([P, 2, 2, P], BF16)
-        gv = gbc[:].rearrange("p q (h r) -> p q h r", r=P)
+        lt = const.tile([P, 2, 3, P], BF16)
+        gt = const.tile([P, 2 * NH], BF16)
+        dg = const.tile([P, 2 * NH, P], BF16)
 
-        def make_rf(qk):
-            rf = work.tile([16, 2 * FW], F32, tag="o", bufs=3, name="rf")
+        def make_dg():
+            pg = ps.tile([P, P], BF16, tag="yn", bufs=6, name="pg")
+            nc.tensor.transpose(pg[:], graw[:], identb[:])
+            nc.vector.tensor_copy(out=gt[:], in_=pg[:, 0:2 * NH])
             nc.vector.tensor_tensor(
-                out=rf[:].rearrange("p (a h r) -> p a h r", a=2, r=FR),
-                in0=gv[0:16, qk, :, 0:FR].unsqueeze(1).to_broadcast([16, 2, NH, FR]),
-                in1=ftx[0:16].rearrange("p a c e -> p a (c e)")[:, :, 0:FR].unsqueeze(2).to_broadcast([16, 2, NH, FR]),
-                op=ALU.mult,
+                out=dg[:], in0=identb[:].unsqueeze(1).to_broadcast([P, 2 * NH, P]),
+                in1=gt[:].unsqueeze(2).to_broadcast([P, 2 * NH, P]), op=ALU.mult,
             )
-            nc.sync.dma_start(out=outs[1][SCR + 16 * qk:SCR + 16 * qk + 16, 0:2 * FW], in_=rf[:])
+
+        def make_lt():
+            for a in range(2):
+                pl = ps.tile([P, 3 * P], F32, tag="yn", bufs=6, name="pl")
+                rows = ftx[:, a].rearrange("k c e -> k (c e)")
+                nc.tensor.matmul(
+                    out=pl[:, 0:2 * P], lhsT=rows, rhs=base[:].rearrange("k s a b -> k (s a b)"), start=True, stop=True
+                )
+                nc.tensor.matmul(out=pl[:, 2 * P:3 * P], lhsT=rows, rhs=identb[:], start=True, stop=True)
+                nc.scalar.copy(out=lt[:, a].rearrange("p s r -> p (s r)"), in_=pl[:])
+
+        rfs = {}
+
+        def rf_compute(qk):
+            rf = work.tile([16, 2 * FW], F32, tag="o", bufs=3, name="rf")
+            for a in range(2):
+                pr = ps.tile([P, NH, FR], F32, tag="yn", bufs=6, name="pr")
+                nc.tensor.matmul(
+                    out=pr[:], lhsT=lt[:, a, 2, :], rhs=dg[:, NH * qk:NH * (qk + 1), 0:FR], start=True, stop=True
+                )
+                nc.scalar.copy(out=rf[:, FW * a:FW * (a + 1)], in_=pr[0:16].rearrange("p h r -> p (h r)"))
+            rfs[qk] = rf
+
+        def rf_store(qk):
+            nc.sync.dma_start(out=outs[1][SCR + 16 * qk:SCR + 16 * qk + 16, 0:2 * FW], in_=rfs[qk][:])
 
         def make_hw(qk, hh, a):
-            nc.vector.tensor_tensor(
-                out=hwtab[:, qk, hh, a].rearrange("p (h r) -> p h r", r=HR),
-                in0=gv[:, qk, :, FR:P],
-                in1=tabs[:, hh, a, FR:P].unsqueeze(1).to_broadcast([P, NH, HR]),
-                op=ALU.mult,
-            )
+            for half in range(2):
+                ph = ps.tile([P, 4, HR], F32, tag="yn", bufs=6, name="ph")
+                h0 = NH * qk + 4 * half
+                nc.tensor.matmul(out=ph[:], lhsT=lt[:, a, hh, :], rhs=dg[:, h0:h0 + 4, FR:P], start=True, stop=True)
+                nc.scalar.copy(
+                    out=hwtab[:, qk, hh, a, 4 * HR * half:4 * HR * (half + 1)], in_=ph[:].rearrange("p h r -> p (h r)")
+                )
 
         ftab = {}
 
@@ -208,13 +235,8 @@ def tile_causalwanselfattention_pa_kernel(
         load_x(2)
         front_x_tile(0, 0)
         front_x_tile(0, 1)
-        pt = ps.tile([P, 2, 256], F32, tag="acc", bufs=2, name="pt")
-        for hh in range(2):
-            nc.tensor.matmul(
-                out=pt[:, hh, :], lhsT=base[hh][:].rearrange("k a b -> k (a b)"),
-                rhs=ftx[:].rearrange("k a c e -> k (a c e)"), start=True, stop=True,
-            )
-        nc.scalar.copy(out=tabs[:].rearrange("p s a r -> p s (a r)"), in_=pt[:])
+        make_dg()
+        make_lt()
         front_x_tile(0, 2)
         front_x_tile(0, 3)
         front_x_quant(0)
@@ -222,6 +244,7 @@ def tile_causalwanselfattention_pa_kernel(
         front_w_head(0, 3)
         load_w(5)
         load_x(3)
+        rf_compute(0)
         front_w_head(0, 4)
         front_w_head(0, 5)
         load_w(6)
@@ -232,25 +255,25 @@ def tile_causalwanselfattention_pa_kernel(
             )
         bcol = const.tile([P, 16], F32)
         nc.vector.tensor_copy(out=bcol[:], in_=pb[:])
+        make_hw(0, 0, 0)
+        make_hw(0, 0, 1)
         front_w_head(0, 6)
         front_w_head(0, 7)
         load_w(7)
-        nc.sync.dma_start(out=gbc[:, 0, :], in_=gq.partition_broadcast(P))
-        nc.sync.dma_start(out=gbc[:, 1, :], in_=gk.partition_broadcast(P))
-        front_w_quant(0)
-        for i in range(4):
-            front_x_tile(1, i)
-        front_x_quant(1)
-        make_rf(0)
+        rf_store(0)
         load_ftab(0, 0)
         load_ftab(1, 0)
-        make_rf(1)
+        front_w_quant(0)
+        make_hw(0, 1, 0)
+        make_hw(0, 1, 1)
+        rf_compute(1)
+        rf_store(1)
         load_ftab(0, 1)
         load_ftab(1, 1)
-        for qk in range(2):
-            for hh in range(2):
-                for a in range(2):
-                    make_hw(qk, hh, a)
+        for i in range(4):
+            front_x_tile(1, i)
+            make_hw(1, i // 2, i % 2)
+        front_x_quant(1)
 
         units = ((0, 0), (1, 0), (0, 1), (1, 1), (2, 0), (2, 1), (3, 0), (3, 1))
 
@@ -319,7 +342,7 @@ def tile_causalwanselfattention_pa_kernel(
             i = 4 * c + ii
             y0 = yn[(j, 0)][:].rearrange("p m r -> p (m r)")
             y1 = yn[(j, 1)][:].rearrange("p m r -> p (m r)")
-            uv = work.tile([P, 2, KDIM], F32, tag="uv", bufs=2, name="uv")
+            uv = work.tile([P, 2, KDIM], F32, tag="uv", bufs=3, name="uv")
             for src, lo, hi, tabv in (
                 (y0[:, 0:FW], 0, FW, ftab[c][:, f2, qk]),
                 (y0[:, FW:CHUNK], FW, CHUNK, hwtab[:, qk, hh, :, 0:CHUNK - FW]),
@@ -343,12 +366,12 @@ def tile_causalwanselfattention_pa_kernel(
             stage_a(2 * i)
             stage_a(2 * i + 1)
             front_w_head(1, 2 * i)
+            front_x_tile(2, i)
             front_w_head(1, 2 * i + 1)
+            front_x_tile(3, i)
+        front_x_quant(2)
         front_w_quant(1)
-        for c in (2, 3):
-            for i in range(4):
-                front_x_tile(c, i)
-            front_x_quant(c)
+        front_x_quant(3)
         for b in range(2):
             t4(0, b)
             sq_bank(0, b)

@@ -148,13 +148,16 @@ def tile_causalwanselfattention_pa_kernel(
             nc.scalar.copy(out=wgw[:, :, FR * h:FR * (h + 1), :], in_=ftv[:, :, 0:FR, :])
             nc.scalar.copy(out=wgw[:, :, FW + HR * h:FW + HR * (h + 1), :], in_=ftv[:, :, FR:P, :])
 
+        def front_w_quant_pass(qk, g):
+            nc.vector.quantize_mx(
+                out=wc[:, qk, g, :].bitcast(FP8X4),
+                scales=ws[:, qk, g, :],
+                in_=wgs[qk][:, g].rearrange("p r t -> p (r t)"),
+            )
+
         def front_w_quant(qk):
             for g in range(2):
-                nc.vector.quantize_mx(
-                    out=wc[:, qk, g, :].bitcast(FP8X4),
-                    scales=ws[:, qk, g, :],
-                    in_=wgs[qk][:, g].rearrange("p r t -> p (r t)"),
-                )
+                front_w_quant_pass(qk, g)
 
         ftx = const.tile([P, 2, 64, 2], BF16)
         nc.vector.tensor_copy(out=ftx[:, 0], in_=raw[:, 0:64].unsqueeze(2).to_broadcast([P, 64, 2]))
@@ -353,8 +356,9 @@ def tile_causalwanselfattention_pa_kernel(
                     scalar=rstd[j][:, 0:1], in1=tabv, op0=ALU.mult, op1=ALU.mult,
                 )
             o = work.tile([P, NH, P], F32, tag="o", bufs=3, name="o")
+            adder = nc.vector if j == 31 else nc.gpsimd
             for lo, hi, r0, r1 in ((0, FW, 0, FR), (FW, KDIM, FR, P)):
-                nc.gpsimd.tensor_tensor(
+                adder.tensor_tensor(
                     out=o[:, :, r0:r1].rearrange("p h (c e) -> p h c e", e=2),
                     in0=uv[:, 0, lo:hi].rearrange("p (h c e) -> p h c e", h=NH, e=2),
                     in1=uv[:, 1, lo:hi].rearrange("p (h c e) -> p h c e", h=NH, e=2)[:, :, :, ::-1],
@@ -369,9 +373,6 @@ def tile_causalwanselfattention_pa_kernel(
             front_x_tile(2, i)
             front_w_head(1, 2 * i + 1)
             front_x_tile(3, i)
-        front_x_quant(2)
-        front_w_quant(1)
-        front_x_quant(3)
         for b in range(2):
             t4(0, b)
             sq_bank(0, b)
@@ -383,6 +384,10 @@ def tile_causalwanselfattention_pa_kernel(
         def at(j, fn, *args):
             later.setdefault(j, []).append((fn, args))
 
+        at(0, front_w_quant_pass, 1, 0)
+        at(1, front_w_quant_pass, 1, 1)
+        at(4, front_x_quant, 2)
+        at(8, front_x_quant, 3)
         at(11, load_ftab, 2, 0)
         at(11, load_ftab, 2, 1)
         at(15, load_ftab, 3, 0)

@@ -63,24 +63,35 @@ def tile_causalwanselfattention_pa_kernel(
         xb = {}
         wraw = {}
 
-        def load_x(c):
-            xb_c = stage.tile([P, 4, KDIM], U8, tag="xb", bufs=4, name="xb")
+        def load_x_part(c, i0, i1):
+            if i0 == 0:
+                xb[c] = stage.tile([P, 4, KDIM], U8, tag="xb", bufs=4, name="xb")
             nc.sync.dma_start(
-                out=xb_c[:], in_=x_bytes[CHUNK * c:CHUNK * (c + 1), :].rearrange("(i p) k -> p i k", p=P)
+                out=xb[c][:, i0:i1, :],
+                in_=x_bytes[CHUNK * c + P * i0:CHUNK * c + P * i1, :].rearrange("(i p) k -> p i k", p=P),
             )
-            xb[c] = xb_c
 
-        def load_w(j):
+        def load_x(c):
+            load_x_part(c, 0, 4)
+
+        def load_w_part(j, m0, m1):
             w = weights[j // 4]
             r0 = 256 * (j % 4)
-            wr = stage.tile([P, 2, KDIM], BF16, tag="wraw", bufs=4, name="wraw")
-            nc.sync.dma_start(out=wr[:], in_=w[r0:r0 + 256, :].rearrange("(m p) k -> p m k", p=P))
-            wraw[j] = wr
+            if m0 == 0:
+                wraw[j] = stage.tile([P, 2, KDIM], BF16, tag="wraw", bufs=4, name="wraw")
+            nc.sync.dma_start(
+                out=wraw[j][:, m0:m1, :], in_=w[r0 + P * m0:r0 + P * m1, :].rearrange("(m p) k -> p m k", p=P)
+            )
 
-        load_w(0)
-        load_x(0)
+        def load_w(j):
+            load_w_part(j, 0, 2)
+
+        load_x_part(0, 0, 1)
         sc_t = const.tile([P, 2, 4], F32)
         nc.sync.dma_start(out=sc_t[:], in_=x_scale.rearrange("o (g p t) -> p (o g) t", p=P, t=4))
+        load_w_part(0, 0, 1)
+        load_x_part(0, 1, 4)
+        load_w_part(0, 1, 2)
         for half, tabl in enumerate((freqs_cos, freqs_sin)):
             for r0, c0, c1 in ((0, 0, 22), (32, 22, 43), (64, 42, 64)):
                 nc.sync.dma_start(out=raw[r0:r0 + 16, 64 * half + c0:64 * half + c1], in_=tabl[:, c0:c1])
@@ -174,17 +185,15 @@ def tile_causalwanselfattention_pa_kernel(
 
         hwtab = const.tile([P, 2, 2, 2, HWW], F32)
         lt = const.tile([P, 2, 3, P], BF16)
-        gt = const.tile([P, 2 * NH], BF16)
+        gt = const.tile([P, 2 * NH], F32)
         dg = const.tile([P, 2 * NH, P], BF16)
 
         def make_dg():
             pg = ps.tile([P, P], BF16, tag="yn", bufs=6, name="pg")
             nc.tensor.transpose(pg[:], graw[:], identb[:])
-            nc.vector.tensor_copy(out=gt[:], in_=pg[:, 0:2 * NH])
-            nc.vector.tensor_tensor(
-                out=dg[:], in0=identb[:].unsqueeze(1).to_broadcast([P, 2 * NH, P]),
-                in1=gt[:].unsqueeze(2).to_broadcast([P, 2 * NH, P]), op=ALU.mult,
-            )
+            nc.scalar.copy(out=gt[:], in_=pg[:, 0:2 * NH])
+            for blk in range(2 * NH):
+                nc.scalar.activation(out=dg[:, blk, :], in_=identb[:], func=ACT.Copy, scale=gt[:, blk:blk + 1])
 
         def make_lt():
             for a in range(2):
@@ -211,9 +220,9 @@ def tile_causalwanselfattention_pa_kernel(
         def rf_store(qk):
             nc.sync.dma_start(out=outs[1][SCR + 16 * qk:SCR + 16 * qk + 16, 0:2 * FW], in_=rfs[qk][:])
 
-        def make_hw(qk, hh, a):
+        def make_hw(qk, hh, a, tag="yn", bufs=6):
             for half in range(2):
-                ph = ps.tile([P, 4, HR], F32, tag="yn", bufs=6, name="ph")
+                ph = ps.tile([P, 4, HR], F32, tag=tag, bufs=bufs, name="ph")
                 h0 = NH * qk + 4 * half
                 nc.tensor.matmul(out=ph[:], lhsT=lt[:, a, hh, :], rhs=dg[:, h0:h0 + 4, FR:P], start=True, stop=True)
                 nc.scalar.copy(
@@ -233,10 +242,10 @@ def tile_causalwanselfattention_pa_kernel(
                 )
 
         front_w_head(0, 0)
+        front_x_tile(0, 0)
         front_w_head(0, 1)
         load_w(4)
         load_x(2)
-        front_x_tile(0, 0)
         front_x_tile(0, 1)
         make_dg()
         make_lt()
@@ -257,7 +266,7 @@ def tile_causalwanselfattention_pa_kernel(
                 out=pb[:, idx:idx + 1], lhsT=bz[:, P * idx:P * (idx + 1)], rhs=identb[:, 0:1], start=True, stop=True
             )
         bcol = const.tile([P, 16], F32)
-        nc.vector.tensor_copy(out=bcol[:], in_=pb[:])
+        nc.scalar.copy(out=bcol[:], in_=pb[:])
         make_hw(0, 0, 0)
         make_hw(0, 0, 1)
         front_w_head(0, 6)
@@ -275,7 +284,6 @@ def tile_causalwanselfattention_pa_kernel(
         load_ftab(1, 1)
         for i in range(4):
             front_x_tile(1, i)
-            make_hw(1, i // 2, i % 2)
         front_x_quant(1)
 
         units = ((0, 0), (1, 0), (0, 1), (1, 1), (2, 0), (2, 1), (3, 0), (3, 1))
@@ -386,6 +394,10 @@ def tile_causalwanselfattention_pa_kernel(
 
         at(0, front_w_quant_pass, 1, 0)
         at(1, front_w_quant_pass, 1, 1)
+        at(2, make_hw, 1, 0, 0, "acc", 2)
+        at(3, make_hw, 1, 0, 1, "acc", 2)
+        at(4, make_hw, 1, 1, 0, "acc", 2)
+        at(5, make_hw, 1, 1, 1, "acc", 2)
         at(4, front_x_quant, 2)
         at(8, front_x_quant, 3)
         at(11, load_ftab, 2, 0)

@@ -48,7 +48,7 @@ def tile_causalwanselfattention_pa_kernel(
         nc.vector.memset(raw[:], 0.0)
         graw = const.tile([P, P], BF16)
         nc.vector.memset(graw[:], 0.0)
-        bz = work.tile([P, 2 * KDIM], BF16, tag="o", bufs=3, name="bz")
+        bz = work.tile([P, 2 * KDIM], BF16, tag="o", bufs=2, name="bz")
         nc.vector.memset(bz[:], 0.0)
         sgn = const.tile([P, 2], F32)
         nc.vector.memset(sgn[:, 0:1], 1.0)
@@ -65,7 +65,7 @@ def tile_causalwanselfattention_pa_kernel(
 
         def load_x_part(c, i0, i1):
             if i0 == 0:
-                xb[c] = stage.tile([P, 4, KDIM], U8, tag="xb", bufs=4, name="xb")
+                xb[c] = stage.tile([P, 4, KDIM], U8, tag="xb", bufs=3, name="xb")
             nc.sync.dma_start(
                 out=xb[c][:, i0:i1, :],
                 in_=x_bytes[CHUNK * c + P * i0:CHUNK * c + P * i1, :].rearrange("(i p) k -> p i k", p=P),
@@ -128,7 +128,7 @@ def tile_causalwanselfattention_pa_kernel(
         def front_x_tile(c, i):
             if i == 0:
                 xgs[c] = stage.tile([P, 2, CHUNK, 4], BF16, tag="xg", bufs=2, align_bytes=64, name="xg")
-            xw = stage.tile([P, KDIM], BF16, tag="xw", bufs=4, name="xw")
+            xw = stage.tile([P, KDIM], BF16, tag="xw", bufs=3, name="xw")
             nc.gpsimd.tensor_copy(out=xw[:], in_=xb[c][:, i, :].bitcast(FP8))
             words = xw[:].bitcast(F32)
             ft = ps.tile([P, 2, P, 2], F32, tag="yn", bufs=6, name="fx")
@@ -208,7 +208,7 @@ def tile_causalwanselfattention_pa_kernel(
         rfs = {}
 
         def rf_compute(qk):
-            rf = work.tile([16, 2 * FW], F32, tag="o", bufs=3, name="rf")
+            rf = work.tile([16, 2 * FW], F32, tag="o", bufs=2, name="rf")
             for a in range(2):
                 pr = ps.tile([P, NH, FR], F32, tag="yn", bufs=6, name="pr")
                 nc.tensor.matmul(
@@ -232,12 +232,11 @@ def tile_causalwanselfattention_pa_kernel(
         ftab = {}
 
         def load_ftab(c, qk):
-            if qk == 0:
-                ftab[c] = work.tile([P, 2, 2, 2, FW], F32, tag="ftab", bufs=2, name="ftab")
+            ftab[(c, qk)] = work.tile([P, 2, 2, FW], F32, tag="ftab", bufs=3, name="ftab")
             for f2 in range(2):
                 row = SCR + 16 * qk + 2 * c + f2
                 nc.sync.dma_start(
-                    out=ftab[c][:, f2, qk].rearrange("p a x -> p (a x)"),
+                    out=ftab[(c, qk)][:, f2].rearrange("p a x -> p (a x)"),
                     in_=outs[1][row:row + 1, 0:2 * FW].rearrange("o x -> (o x)").partition_broadcast(P),
                 )
 
@@ -281,7 +280,6 @@ def tile_causalwanselfattention_pa_kernel(
         rf_compute(1)
         rf_store(1)
         load_ftab(0, 1)
-        load_ftab(1, 1)
         for i in range(4):
             front_x_tile(1, i)
         front_x_quant(1)
@@ -346,33 +344,47 @@ def tile_causalwanselfattention_pa_kernel(
             nc.scalar.activation(out=rs[:], in_=means[j][:], func=ACT.Abs_reciprocal_sqrt)
             rstd[j] = rs
 
+        uvs = {}
+        o2s = {}
+
+        def add_and_store(adder, j0, t0, t1):
+            c, qk = units[j0 // 4]
+            i0 = 4 * c + j0 % 4 + t0
+            for lo, hi, r0, r1 in ((0, FW, 0, FR), (FW, KDIM, FR, P)):
+                adder.tensor_tensor(
+                    out=o2s[j0][:, t0:t1, :, r0:r1].rearrange("p t h (c e) -> p t h c e", e=2),
+                    in0=uvs[j0][:, t0:t1, 0, lo:hi].rearrange("p t (h c e) -> p t h c e", h=NH, e=2),
+                    in1=uvs[j0][:, t0:t1, 1, lo:hi].rearrange("p t (h c e) -> p t h c e", h=NH, e=2)[:, :, :, :, ::-1],
+                    op=ALU.add,
+                )
+            nc.sync.dma_start(
+                out=outs[qk][P * i0:P * (i0 + t1 - t0), :].rearrange("(t p) x -> p t x", p=P),
+                in_=o2s[j0][:, t0:t1].rearrange("p t h r -> p t (h r)"),
+            )
+
         def rot(j):
             unit, ii = j // 4, j % 4
             c, qk = units[unit]
             f2, hh = ii // 2, ii % 2
-            i = 4 * c + ii
+            j0, t = j - j % 2, j % 2
             y0 = yn[(j, 0)][:].rearrange("p m r -> p (m r)")
             y1 = yn[(j, 1)][:].rearrange("p m r -> p (m r)")
-            uv = work.tile([P, 2, KDIM], F32, tag="uv", bufs=3, name="uv")
+            if t == 0:
+                uvs[j0] = work.tile([P, 2, 2, KDIM], F32, tag="uv", bufs=2, name="uv")
+                o2s[j0] = work.tile([P, 2, NH, P], F32, tag="o", bufs=2, name="o")
             for src, lo, hi, tabv in (
-                (y0[:, 0:FW], 0, FW, ftab[c][:, f2, qk]),
+                (y0[:, 0:FW], 0, FW, ftab[(c, qk)][:, f2]),
                 (y0[:, FW:CHUNK], FW, CHUNK, hwtab[:, qk, hh, :, 0:CHUNK - FW]),
                 (y1, CHUNK, KDIM, hwtab[:, qk, hh, :, CHUNK - FW:HWW]),
             ):
                 nc.vector.scalar_tensor_tensor(
-                    out=uv[:, :, lo:hi], in0=src.unsqueeze(1).to_broadcast([P, 2, hi - lo]),
+                    out=uvs[j0][:, t, :, lo:hi], in0=src.unsqueeze(1).to_broadcast([P, 2, hi - lo]),
                     scalar=rstd[j][:, 0:1], in1=tabv, op0=ALU.mult, op1=ALU.mult,
                 )
-            o = work.tile([P, NH, P], F32, tag="o", bufs=3, name="o")
-            adder = nc.vector if j == 31 else nc.gpsimd
-            for lo, hi, r0, r1 in ((0, FW, 0, FR), (FW, KDIM, FR, P)):
-                adder.tensor_tensor(
-                    out=o[:, :, r0:r1].rearrange("p h (c e) -> p h c e", e=2),
-                    in0=uv[:, 0, lo:hi].rearrange("p (h c e) -> p h c e", h=NH, e=2),
-                    in1=uv[:, 1, lo:hi].rearrange("p (h c e) -> p h c e", h=NH, e=2)[:, :, :, ::-1],
-                    op=ALU.add,
-                )
-            nc.sync.dma_start(out=outs[qk][P * i:P * (i + 1), :], in_=o[:].rearrange("p h r -> p (h r)"))
+            if j0 in (0, 30):
+                add_and_store(nc.vector if j == 31 else nc.gpsimd, j0, t, t + 1)
+            elif t == 1:
+                add_and_store(nc.gpsimd, j0, 0, 2)
 
         for i in range(4):
             stage_a(2 * i)
@@ -400,10 +412,8 @@ def tile_causalwanselfattention_pa_kernel(
         at(5, make_hw, 1, 1, 1, "acc", 2)
         at(4, front_x_quant, 2)
         at(8, front_x_quant, 3)
-        at(11, load_ftab, 2, 0)
-        at(11, load_ftab, 2, 1)
-        at(15, load_ftab, 3, 0)
-        at(15, load_ftab, 3, 1)
+        for unit in range(3, 8):
+            at(4 * unit - 9, load_ftab, *units[unit])
 
         nxt = 8
         for j in range(32):

@@ -393,6 +393,9 @@ def tile_causalwanselfattention_pa_kernel(
             front_x_tile(2, i)
             front_w_head(1, 2 * i + 1)
             front_x_tile(3, i)
+        front_x_quant(2)
+        front_w_quant(1)
+        front_x_quant(3)
         for b in range(2):
             t4(0, b)
             sq_bank(0, b)
@@ -404,14 +407,10 @@ def tile_causalwanselfattention_pa_kernel(
         def at(j, fn, *args):
             later.setdefault(j, []).append((fn, args))
 
-        at(0, front_w_quant_pass, 1, 0)
-        at(1, front_w_quant_pass, 1, 1)
         at(2, make_hw, 1, 0, 0, "acc", 2)
         at(3, make_hw, 1, 0, 1, "acc", 2)
         at(4, make_hw, 1, 1, 0, "acc", 2)
         at(5, make_hw, 1, 1, 1, "acc", 2)
-        at(4, front_x_quant, 2)
-        at(8, front_x_quant, 3)
         for unit in range(3, 8):
             at(4 * unit - 9, load_ftab, *units[unit])
 

@@ -256,6 +256,8 @@ def tile_causalwanselfattention_pa_kernel(
         load_w(5)
         load_x(3)
         rf_compute(0)
+        rf_store(0)
+        load_ftab(0, 0)
         front_w_head(0, 4)
         front_w_head(0, 5)
         load_w(6)
@@ -271,8 +273,6 @@ def tile_causalwanselfattention_pa_kernel(
         front_w_head(0, 6)
         front_w_head(0, 7)
         load_w(7)
-        rf_store(0)
-        load_ftab(0, 0)
         load_ftab(1, 0)
         front_w_quant(0)
         make_hw(0, 1, 0)

from contextlib import ExitStack

import concourse.mybir as mybir
from concourse.masks import make_identity

F32 = mybir.dt.float32
BF16 = mybir.dt.bfloat16
U32 = mybir.dt.uint32
U8 = mybir.dt.uint8
FP8 = mybir.dt.float8_e4m3fn
FP8X4 = mybir.dt.float8_e4m3fn_x4
ALU = mybir.AluOpType
ACT = mybir.ActivationFunctionType

P = 128
KDIM = 1024
CHUNK = 512
NCHUNK = 4
NH = 8
EPS = 1e-06
FR = 44
HR = 84
FW = NH * FR
HWW = NH * HR
SCR = 1920

FLOPS = 2 * 2048 * 2048 * 1024


def tile_causalwanselfattention_pa_kernel(
    tc, x_bytes, x_scale, Wq, bq, Wk, bk, gq, gk, freqs_cos, freqs_sin, out_0, out_1
):
    nc = tc.nc
    outs = (out_0.rearrange("t n d -> t (n d)"), out_1.rearrange("t n d -> t (n d)"))
    weights = (Wq, Wk)

    with ExitStack() as ctx:
        const = ctx.enter_context(tc.tile_pool(name="const", bufs=1))
        keep = ctx.enter_context(tc.tile_pool(name="keep", bufs=1))
        stage = ctx.enter_context(tc.tile_pool(name="stage", bufs=2))
        ypool = ctx.enter_context(tc.tile_pool(name="ypool", bufs=2))
        work = ctx.enter_context(tc.tile_pool(name="work", bufs=2))
        stats = ctx.enter_context(tc.tile_pool(name="stats", bufs=4))
        ps = ctx.enter_context(tc.psum_pool(name="ps", bufs=2))
        ctx.enter_context(tc.manual_schedule(engines={mybir.EngineType.PE, mybir.EngineType.Activation, mybir.EngineType.SP}))

        raw = const.tile([P, P], BF16)
        nc.vector.memset(raw[:], 0.0)
        graw = const.tile([P, P], BF16)
        nc.vector.memset(graw[:], 0.0)
        bz = work.tile([P, 2 * KDIM], BF16, tag="o", bufs=2, name="bz")
        nc.vector.memset(bz[:], 0.0)
        sgn = const.tile([P, 2], F32)
        nc.vector.memset(sgn[:, 0:1], 1.0)
        nc.vector.memset(sgn[:, 1:2], -1.0)
        warm = const.tile([P, 1], F32)
        nc.scalar.activation(out=warm[:], in_=sgn[:, 0:1], func=ACT.Abs_reciprocal_sqrt)
        identf = const.tile([P, P], F32)
        make_identity(nc, identf[:])
        identb = const.tile([P, P], BF16)
        make_identity(nc, identb[:])

        xb = {}
        wraw = {}

        def load_x_part(c, i0, i1):
            if i0 == 0:
                xb[c] = stage.tile([P, 4, KDIM], U8, tag="xb", bufs=3, name="xb")
            nc.sync.dma_start(
                out=xb[c][:, i0:i1, :],
                in_=x_bytes[CHUNK * c + P * i0:CHUNK * c + P * i1, :].rearrange("(i p) k -> p i k", p=P),
            )

        def load_x(c):
            load_x_part(c, 0, 4)

        def load_w_part(j, m0, m1):
            w = weights[j // 4]
            r0 = 256 * (j % 4)
            if m0 == 0:
                wraw[j] = stage.tile([P, 2, KDIM], BF16, tag="wraw", bufs=4, name="wraw")
            nc.sync.dma_start(
                out=wraw[j][:, m0:m1, :], in_=w[r0 + P * m0:r0 + P * m1, :].rearrange("(m p) k -> p m k", p=P)
            )

        def load_w(j):
            load_w_part(j, 0, 2)

        load_x_part(0, 0, 1)
        sc_t = const.tile([P, 2, 4], F32)
        nc.sync.dma_start(out=sc_t[:], in_=x_scale.rearrange("o (g p t) -> p (o g) t", p=P, t=4))
        load_w_part(0, 0, 1)
        load_x_part(0, 1, 4)
        load_w_part(0, 1, 2)
        for half, tabl in enumerate((freqs_cos, freqs_sin)):
            for r0, c0, c1 in ((0, 0, 22), (32, 22, 43), (64, 42, 64)):
                nc.sync.dma_start(out=raw[r0:r0 + 16, 64 * half + c0:64 * half + c1], in_=tabl[:, c0:c1])
            nc.vector.memset(raw[64:80, 64 * half + 42:64 * half + 43], 0.0)
        for qk, vec in enumerate((gq, gk)):
            nc.sync.dma_start(out=graw[NH * qk:NH * (qk + 1), :], in_=vec.rearrange("(h r) -> h r", r=P))
        for j in range(1, 4):
            load_w(j)
        for qk, vec in enumerate((bq, bk)):
            v3 = vec.rearrange("(o h r) -> o h r", o=1, r=P)
            nc.sync.dma_start(
                out=bz[0:1, KDIM * qk:KDIM * qk + FW].rearrange("o (h r) -> o h r", r=FR), in_=v3[:, :, 0:FR]
            )
            nc.sync.dma_start(
                out=bz[0:1, KDIM * qk + FW:KDIM * (qk + 1)].rearrange("o (h r) -> o h r", r=HR), in_=v3[:, :, FR:P]
            )
        load_x(1)

        xc = keep.tile([P, NCHUNK, 2, CHUNK], U32, align_bytes=64)
        xs = keep.tile([P, NCHUNK, 2, CHUNK], U8, align_bytes=64)
        wc = keep.tile([P, 2, 2, KDIM], U32, align_bytes=64)
        ws = keep.tile([P, 2, 2, KDIM], U8, align_bytes=64)

        def turn(rows_bf16):
            words = rows_bf16.bitcast(F32)
            ft = ps.tile([P, 4, P], F32, tag="yn", bufs=6, name="ft")
            for g in range(2):
                for u in range(2):
                    nc.tensor.transpose(ft[:, 2 * g + u, :], words[:, 256 * g + u:256 * (g + 1):2], identf[:])
            return ft[:].rearrange("p (g u) r -> p g r u", u=2)

        xgs = {}

        def front_x_tile(c, i):
            if i == 0:
                xgs[c] = stage.tile([P, 2, CHUNK, 4], BF16, tag="xg", bufs=2, align_bytes=64, name="xg")
            xw = stage.tile([P, KDIM], BF16, tag="xw", bufs=3, name="xw")
            nc.gpsimd.tensor_copy(out=xw[:], in_=xb[c][:, i, :].bitcast(FP8))
            words = xw[:].bitcast(F32)
            ft = ps.tile([P, 2, P, 2], F32, tag="yn", bufs=6, name="fx")
            for g in range(2):
                for u in range(2):
                    nc.tensor.transpose(ft[:, g, :, u], words[:, 256 * g + u:256 * (g + 1):2], identf[:])
            nc.vector.tensor_tensor(
                out=xgs[c][:, :, P * i:P * (i + 1), :],
                in0=ft[:].rearrange("p g r u -> p (g r u)").bitcast(BF16).rearrange("p (g r t) -> p g r t", g=2, t=4),
                in1=sc_t[:].unsqueeze(2).to_broadcast([P, 2, P, 4]),
                op=ALU.mult,
            )

        def front_x_quant(c):
            nc.vector.quantize_mx(
                out=xc[:, c].rearrange("p g n -> p (g n)").bitcast(FP8X4),
                scales=xs[:, c].rearrange("p g n -> p (g n)"),
                in_=xgs[c][:].rearrange("p g r t -> p (g r t)"),
            )

        wgs = {}

        def front_w_head(qk, h):
            if h == 0:
                wgs[qk] = stage.tile([P, 2, KDIM, 4], BF16, tag="wg", bufs=1, align_bytes=64, name="wg")
            wgw = wgs[qk][:].bitcast(F32)
            ftv = turn(wraw[4 * qk + h // 2][:, h % 2, :])
            nc.scalar.copy(out=wgw[:, :, FR * h:FR * (h + 1), :], in_=ftv[:, :, 0:FR, :])
            nc.scalar.copy(out=wgw[:, :, FW + HR * h:FW + HR * (h + 1), :], in_=ftv[:, :, FR:P, :])

        def front_w_quant_pass(qk, g):
            nc.vector.quantize_mx(
                out=wc[:, qk, g, :].bitcast(FP8X4),
                scales=ws[:, qk, g, :],
                in_=wgs[qk][:, g].rearrange("p r t -> p (r t)"),
            )

        def front_w_quant(qk):
            for g in range(2):
                front_w_quant_pass(qk, g)

        ftx = const.tile([P, 2, 64, 2], BF16)
        nc.vector.tensor_copy(out=ftx[:, 0], in_=raw[:, 0:64].unsqueeze(2).to_broadcast([P, 64, 2]))
        nc.vector.tensor_tensor(
            out=ftx[:, 1], in0=raw[:, 64:128].unsqueeze(2).to_broadcast([P, 64, 2]),
            in1=sgn[:].unsqueeze(1).to_broadcast([P, 64, 2]), op=ALU.mult,
        )
        base = const.tile([P, 2, 8, 16], BF16)
        for hh in range(2):
            nc.vector.tensor_tensor(
                out=base[:, hh], in0=identb[:, 32 + 8 * hh:40 + 8 * hh].unsqueeze(2).to_broadcast([P, 8, 16]),
                in1=identb[:, 64:80].unsqueeze(1).to_broadcast([P, 8, 16]), op=ALU.add,
            )

        hwtab = const.tile([P, 2, 2, 2, HWW], F32)
        lt = const.tile([P, 2, 3, P], BF16)
        gt = const.tile([P, 2 * NH], F32)
        dg = const.tile([P, 2 * NH, P], BF16)

        def make_dg():
            pg = ps.tile([P, P], BF16, tag="yn", bufs=6, name="pg")
            nc.tensor.transpose(pg[:], graw[:], identb[:])
            nc.scalar.copy(out=gt[:], in_=pg[:, 0:2 * NH])
            for blk in range(2 * NH):
                nc.scalar.activation(out=dg[:, blk, :], in_=identb[:], func=ACT.Copy, scale=gt[:, blk:blk + 1])

        def make_lt():
            for a in range(2):
                pl = ps.tile([P, 3 * P], F32, tag="yn", bufs=6, name="pl")
                rows = ftx[:, a].rearrange("k c e -> k (c e)")
                nc.tensor.matmul(
                    out=pl[:, 0:2 * P], lhsT=rows, rhs=base[:].rearrange("k s a b -> k (s a b)"), start=True, stop=True
                )
                nc.tensor.matmul(out=pl[:, 2 * P:3 * P], lhsT=rows, rhs=identb[:], start=True, stop=True)
                nc.scalar.copy(out=lt[:, a].rearrange("p s r -> p (s r)"), in_=pl[:])

        rfs = {}

        def rf_compute(qk):
            rf = work.tile([16, 2 * FW], F32, tag="o", bufs=2, name="rf")
            for a in range(2):
                pr = ps.tile([P, NH, FR], F32, tag="yn", bufs=6, name="pr")
                nc.tensor.matmul(
                    out=pr[:], lhsT=lt[:, a, 2, :], rhs=dg[:, NH * qk:NH * (qk + 1), 0:FR], start=True, stop=True
                )
                nc.scalar.copy(out=rf[:, FW * a:FW * (a + 1)], in_=pr[0:16].rearrange("p h r -> p (h r)"))
            rfs[qk] = rf

        def rf_store(qk):
            nc.sync.dma_start(out=outs[1][SCR + 16 * qk:SCR + 16 * qk + 16, 0:2 * FW], in_=rfs[qk][:])

        def make_hw(qk, hh, a, tag="yn", bufs=6):
            for half in range(2):
                ph = ps.tile([P, 4, HR], F32, tag=tag, bufs=bufs, name="ph")
                h0 = NH * qk + 4 * half
                nc.tensor.matmul(out=ph[:], lhsT=lt[:, a, hh, :], rhs=dg[:, h0:h0 + 4, FR:P], start=True, stop=True)
                nc.scalar.copy(
                    out=hwtab[:, qk, hh, a, 4 * HR * half:4 * HR * (half + 1)], in_=ph[:].rearrange("p h r -> p (h r)")
                )

        ftab = {}

        def load_ftab(c, qk):
            ftab[(c, qk)] = work.tile([P, 2, 2, FW], F32, tag="ftab", bufs=3, name="ftab")
            for f2 in range(2):
                row = SCR + 16 * qk + 2 * c + f2
                nc.sync.dma_start(
                    out=ftab[(c, qk)][:, f2].rearrange("p a x -> p (a x)"),
                    in_=outs[1][row:row + 1, 0:2 * FW].rearrange("o x -> (o x)").partition_broadcast(P),
                )

        front_w_head(0, 0)
        front_x_tile(0, 0)
        front_w_head(0, 1)
        load_w(4)
        load_x(2)
        front_x_tile(0, 1)
        make_dg()
        make_lt()
        front_x_tile(0, 2)
        front_x_tile(0, 3)
        front_x_quant(0)
        front_w_head(0, 2)
        front_w_head(0, 3)
        load_w(5)
        load_x(3)
        rf_compute(0)
        rf_store(0)
        load_ftab(0, 0)
        front_w_head(0, 4)
        front_w_head(0, 5)
        load_w(6)
        pb = ps.tile([P, 16], F32, tag="acc", bufs=2, name="pb")
        for idx in range(16):
            nc.tensor.matmul(
                out=pb[:, idx:idx + 1], lhsT=bz[:, P * idx:P * (idx + 1)], rhs=identb[:, 0:1], start=True, stop=True
            )
        bcol = const.tile([P, 16], F32)
        nc.scalar.copy(out=bcol[:], in_=pb[:])
        make_hw(0, 0, 0)
        make_hw(0, 0, 1)
        front_w_head(0, 6)
        front_w_head(0, 7)
        load_w(7)
        load_ftab(1, 0)
        front_w_quant(0)
        make_hw(0, 1, 0)
        make_hw(0, 1, 1)
        rf_compute(1)
        rf_store(1)
        load_ftab(0, 1)
        for i in range(4):
            front_x_tile(1, i)
        front_x_quant(1)

        units = ((0, 0), (1, 0), (0, 1), (1, 1), (2, 0), (2, 1), (3, 0), (3, 1))

        yT = {}

        def stage_a(a):
            unit, m = a // 8, a % 8
            c, qk = units[unit]
            acc = ps.tile([P, CHUNK], F32, tag="acc", bufs=2, name="acc")
            for g in range(2):
                nc.tensor.matmul_mx(
                    out=acc[:],
                    lhsT=wc[:, qk, g, P * m:P * (m + 1)].bitcast(FP8X4),
                    lhsT_scale=ws[:, qk, g, P * m:P * (m + 1)],
                    rhs=xc[:, c, g, :].bitcast(FP8X4),
                    rhs_scale=xs[:, c, g, :],
                    start=(g == 0),
                    stop=(g == 1),
                )
            yt = ypool.tile([P, CHUNK], F32, tag="yT", bufs=16, name="yT")
            nc.scalar.activation(
                out=yt[:], in_=acc[:], func=ACT.Identity, bias=bcol[:, 8 * qk + m:8 * qk + m + 1], scale=1.0
            )
            yT[(unit, m)] = yt

        yn = {}
        rstd = {}

        def t4(j, b):
            unit, ii = j // 4, j % 4
            y = ps.tile([P, 4, P], F32, tag="yn", bufs=6, name="yn")
            for mm in range(4):
                nc.tensor.transpose(y[:, mm, :], yT[(unit, 4 * b + mm)][:, P * ii:P * (ii + 1)], identf[:])
            yn[(j, b)] = y

        sums = {}

        def sq_bank(j, b):
            if b == 0:
                sums[j] = stats.tile([P, 2], F32, name="s2")
            junk = work.tile([P, CHUNK], BF16, tag="junk", bufs=2, name="junk")
            nc.scalar.activation(
                out=junk[:], in_=yn[(j, b)][:].rearrange("p m r -> p (m r)"), func=ACT.Square,
                scale=1.0 / 32.0, accum_out=sums[j][:, b:b + 1],
            )

        means = {}

        def sq_sum(j):
            j2 = stats.tile([P, 2], F32, name="j2")
            ms = stats.tile([P, 1], F32, name="ms")
            nc.scalar.activation(
                out=j2[:], in_=sums[j][:], func=ACT.Identity, bias=0.5 * EPS, scale=1.0, accum_out=ms[:]
            )
            means[j] = ms

        def sq_root(j):
            rs = stats.tile([P, 1], F32, name="rs")
            nc.scalar.activation(out=rs[:], in_=means[j][:], func=ACT.Abs_reciprocal_sqrt)
            rstd[j] = rs

        uvs = {}
        o2s = {}

        def add_and_store(adder, j0, t0, t1):
            c, qk = units[j0 // 4]
            i0 = 4 * c + j0 % 4 + t0
            for lo, hi, r0, r1 in ((0, FW, 0, FR), (FW, KDIM, FR, P)):
                adder.tensor_tensor(
                    out=o2s[j0][:, t0:t1, :, r0:r1].rearrange("p t h (c e) -> p t h c e", e=2),
                    in0=uvs[j0][:, t0:t1, 0, lo:hi].rearrange("p t (h c e) -> p t h c e", h=NH, e=2),
                    in1=uvs[j0][:, t0:t1, 1, lo:hi].rearrange("p t (h c e) -> p t h c e", h=NH, e=2)[:, :, :, :, ::-1],
                    op=ALU.add,
                )
            nc.sync.dma_start(
                out=outs[qk][P * i0:P * (i0 + t1 - t0), :].rearrange("(t p) x -> p t x", p=P),
                in_=o2s[j0][:, t0:t1].rearrange("p t h r -> p t (h r)"),
            )

        def rot(j):
            unit, ii = j // 4, j % 4
            c, qk = units[unit]
            f2, hh = ii // 2, ii % 2
            j0, t = j - j % 2, j % 2
            y0 = yn[(j, 0)][:].rearrange("p m r -> p (m r)")
            y1 = yn[(j, 1)][:].rearrange("p m r -> p (m r)")
            if t == 0:
                uvs[j0] = work.tile([P, 2, 2, KDIM], F32, tag="uv", bufs=2, name="uv")
                o2s[j0] = work.tile([P, 2, NH, P], F32, tag="o", bufs=2, name="o")
            for src, lo, hi, tabv in (
                (y0[:, 0:FW], 0, FW, ftab[(c, qk)][:, f2]),
                (y0[:, FW:CHUNK], FW, CHUNK, hwtab[:, qk, hh, :, 0:CHUNK - FW]),
                (y1, CHUNK, KDIM, hwtab[:, qk, hh, :, CHUNK - FW:HWW]),
            ):
                nc.vector.scalar_tensor_tensor(
                    out=uvs[j0][:, t, :, lo:hi], in0=src.unsqueeze(1).to_broadcast([P, 2, hi - lo]),
                    scalar=rstd[j][:, 0:1], in1=tabv, op0=ALU.mult, op1=ALU.mult,
                )
            if j0 in (0, 30):
                add_and_store(nc.vector if j == 31 else nc.gpsimd, j0, t, t + 1)
            elif t == 1:
                add_and_store(nc.gpsimd, j0, 0, 2)

        for i in range(4):
            stage_a(2 * i)
            stage_a(2 * i + 1)
            front_w_head(1, 2 * i)
            front_x_tile(2, i)
            front_w_head(1, 2 * i + 1)
            front_x_tile(3, i)
        front_x_quant(2)
        front_w_quant(1)
        front_x_quant(3)
        for b in range(2):
            t4(0, b)
            sq_bank(0, b)
        sq_sum(0)
        sq_root(0)

        later = {}

        def at(j, fn, *args):
            later.setdefault(j, []).append((fn, args))

        at(2, make_hw, 1, 0, 0, "acc", 2)
        at(3, make_hw, 1, 0, 1, "acc", 2)
        at(4, make_hw, 1, 1, 0, "acc", 2)
        at(5, make_hw, 1, 1, 1, "acc", 2)
        for unit in range(3, 8):
            at(4 * unit - 9, load_ftab, *units[unit])

        nxt = 8
        for j in range(32):
            todo = []
            while nxt < 64 and nxt < 2 * j + 12 and len(todo) < 3:
                todo.append(nxt)
                nxt += 1
            if j + 1 < 32:
                for b in range(2):
                    t4(j + 1, b)
                    sq_bank(j + 1, b)
            for a in todo[0:1]:
                stage_a(a)
            if j + 1 < 32:
                sq_sum(j + 1)
            for a in todo[1:]:
                stage_a(a)
            if j + 1 < 32:
                sq_root(j + 1)
            rot(j)
            for fn, args in later.get(j, ()):
                fn(*args)
